import numpy as np
import ml_dtypes


def mxq(x, axis, fmt="e4m3"):
    dtype, down = {"e4m3": (ml_dtypes.float8_e4m3fn, 7), "e5m2": (ml_dtypes.float8_e5m2, 14)}[fmt]
    v = np.moveaxis(np.asarray(x, np.float32).astype(ml_dtypes.bfloat16).astype(np.float64), axis, -1)
    blocks = v.reshape(v.shape[:-1] + (-1, 32))
    amax = np.abs(blocks).max(-1, keepdims=True)
    byte = np.maximum(np.where(amax > 0, np.frexp(amax)[1] - 1 + 127, 0) - down, 1)
    scale = np.exp2(byte - 127.0)
    codes = (blocks / scale).astype(np.float32).astype(dtype).astype(np.float64)
    return np.moveaxis((codes * scale).reshape(v.shape), -1, axis)


WIDE = False


def mx_kscale(k):
    if not WIDE:
        return np.ones(k)
    levels = np.array([10, -10, 5, -5, 0])
    a = np.random.permutation(np.resize(levels, k // 512 * 4)).reshape(k // 512, 4)
    idx = np.arange(k)
    return np.exp2(a[idx // 512, idx % 128 // 32])


BF16 = ml_dtypes.bfloat16


def bf(x):
    return np.asarray(x, np.float32).astype(BF16)


def f64(x):
    return np.asarray(x).astype(np.float64)


E2M1 = np.array([0.0, 0.5, 1.0, 1.5, 2.0, 3.0, 4.0, 6.0, -0.0, -0.5, -1.0, -1.5, -2.0, -3.0, -4.0, -6.0])


def pack_weight(w, fmt):
    k, n = w.shape
    w = f64(bf(w)).reshape(k // 32, 32, n)
    amax = np.abs(w).max(1)
    if fmt == "e4m3":
        byte = np.frexp(amax)[1] - 1 + 127 - 7
    else:
        mant, ex = np.frexp(amax / 6.0)
        byte = np.where(mant > 0.5, ex, ex - 1) + 127
    byte = np.clip(np.where(amax > 0, byte, 1), 1, 254)
    scaled = (w * np.exp2(127.0 - byte)[:, None, :]).reshape(k, n).astype(np.float32)
    by_word = np.ascontiguousarray(scaled.reshape(k // 512, 128, 4, n).transpose(0, 1, 3, 2))
    if fmt == "e4m3":
        words = by_word.astype(ml_dtypes.float8_e4m3fn).view(np.uint8)
    else:
        c = by_word.astype(ml_dtypes.float4_e2m1fn).view(np.uint8) & 0xF
        words = c[..., 0::2] | (c[..., 1::2] << 4)
    return np.ascontiguousarray(words), np.ascontiguousarray(byte.astype(np.uint8).reshape(k // 512, 16, n))


def unpack_weight(words, scales, fmt):
    g, p, n, _ = words.shape
    if fmt == "e4m3":
        vals = np.ascontiguousarray(words).view(ml_dtypes.float8_e4m3fn).astype(np.float64)
    else:
        nib = np.empty((g, p, n, 4), np.uint8)
        nib[..., 0::2] = words & 0xF
        nib[..., 1::2] = words >> 4
        vals = E2M1[nib]
    vals = vals * np.repeat(np.exp2(scales.astype(np.float64) - 127.0), 8, axis=1)[..., None]
    return vals.transpose(0, 1, 3, 2).reshape(g * 512, n)

def pack4(w):
    words, scales = pack_weight(w, "e2m1")
    return words.reshape(words.shape[0], 128, -1), scales


def unpack4(words, scales):
    return unpack_weight(words.reshape(words.shape[0], 128, -1, 2), scales, "e2m1")


B, N, D = 4, 512, 512
C = 2 * D
EPS_BN = 1e-5
NEG_SLOPE = 0.01


def bn_lrelu(x, g, b):
    mean = np.mean(x, axis=(0, 2), keepdims=True)
    var = np.var(x, axis=(0, 2), keepdims=True)
    y = (x - mean) / np.sqrt(var + EPS_BN) * g[None, :, None] + b[None, :, None]
    return np.where(y >= 0, y, NEG_SLOPE * y)


def setup_inputs():
    s = mx_kscale(C)
    v = np.random.standard_normal((B, C, N))
    w2 = np.random.standard_normal((D, C)) / np.sqrt(C) / s[None, :]
    words, scales = pack4(np.ascontiguousarray(w2.T))
    return {"h1": bf(np.where(v >= 0, v, NEG_SLOPE * v) * s[None, :, None]),
            "W2_words": words,
            "W2_scales": scales,
            "g2": bf(1.0 + 0.2 * np.random.standard_normal(D)),
            "b2": bf(0.3 * np.random.standard_normal(D))}


def reference(h1, W2_words, W2_scales, g2, b2):
    z = unpack4(W2_words, W2_scales).T @ mxq(f64(h1), 1, "e4m3")
    return np.swapaxes(bn_lrelu(z, f64(g2), f64(b2)), 1, 2)

@@ -1,0 +1,205 @@
+from contextlib import ExitStack
+
+import concourse.masks as masks
+import concourse.mybir as mybir
+
+BF16 = mybir.dt.bfloat16
+F32 = mybir.dt.float32
+I32 = mybir.dt.int32
+U8 = mybir.dt.uint8
+U32 = mybir.dt.uint32
+FP8X4 = mybir.dt.float8_e4m3fn_x4
+FP4X4 = mybir.dt.float4_e2m1fn_x4
+ALU = mybir.AluOpType
+ACT = mybir.ActivationFunctionType
+
+P = 128
+PACK = 4
+K_PASS = P * PACK
+
+GRAPHS, CHANNELS_IN, NODES, CHANNELS_OUT = 4, 1024, 512, 512
+PASSES = CHANNELS_IN // K_PASS
+O_TILES = CHANNELS_OUT // P
+N_TILES = NODES // P
+BANKS = O_TILES * GRAPHS
+EPS_BN = 1e-5
+NEG_SLOPE = 0.01
+
+FLOPS = 2 * GRAPHS * NODES * CHANNELS_IN * CHANNELS_OUT
+
+RUN = 4
+RUNS = NODES // RUN
+VECTOR_RUNS = 56
+LAG = 5
+
+
+def tile_yuyipointupdate_pb_kernel(tc, h1, W2_words, W2_scales, g2, b2, out):
+    nc = tc.nc
+    with ExitStack() as ctx:
+        keep = ctx.enter_context(tc.tile_pool(name="keep", bufs=1))
+        group_pool = ctx.enter_context(tc.tile_pool(name="group", bufs=3))
+        work = ctx.enter_context(tc.tile_pool(name="work", bufs=4))
+        small = ctx.enter_context(tc.tile_pool(name="small", bufs=2))
+        z_pool = ctx.enter_context(tc.psum_pool(name="z", bufs=LAG + 1))
+        t_pool = ctx.enter_context(tc.psum_pool(name="t", bufs=2))
+        ctx.enter_context(tc.manual_schedule())
+
+        w_planes = keep.tile([P, PASSES, CHANNELS_OUT], U8, name="w_planes", align_bytes=64)
+        nc.vector.memset(w_planes[:].bitcast(I32), 0)
+        gb_rows = keep.tile([2 * O_TILES, P], BF16, name="gb_rows")
+        nc.scalar.dma_start(out=gb_rows[0:O_TILES, :], in_=g2.rearrange("(t m) -> t m", m=P))
+        nc.scalar.dma_start(out=gb_rows[O_TILES : 2 * O_TILES, :], in_=b2.rearrange("(t m) -> t m", m=P))
+        for quadrant in range(4):
+            nc.scalar.dma_start(
+                out=w_planes[32 * quadrant : 32 * quadrant + 4, :, :].bitcast(F32),
+                in_=W2_scales.bitcast(F32)[:, 4 * quadrant : 4 * quadrant + 4, :].rearrange("g r m -> r g m"),
+            )
+
+        raw = {}
+
+        def load_graph(b):
+            for g in range(PASSES):
+                raw[b, g] = keep.tile([P, PACK, NODES], BF16, name="raw_%d_%d" % (b, g))
+                rows = h1[b, g * K_PASS : (g + 1) * K_PASS, :]
+                nc.sync.dma_start(out=raw[b, g][:], in_=rows.rearrange("(p t) n -> p t n", t=PACK))
+
+        load_graph(0)
+        w_words = keep.tile([P, PASSES, 2 * CHANNELS_OUT], U8, name="w_words", align_bytes=64)
+        nc.sync.dma_start(out=w_words[:].bitcast(I32), in_=W2_words.bitcast(I32).rearrange("g p m -> p g m"))
+        for b in range(1, GRAPHS):
+            load_graph(b)
+
+        minus_half = keep.tile([P, 1], F32, name="minus_half")
+        nc.gpsimd.memset(minus_half[:], -0.5)
+        identity = keep.tile([P, P], F32, name="identity")
+        masks.make_identity(nc, identity[:])
+
+        gb_square = keep.tile([P, P], F32, name="gb_square")
+        nc.vector.memset(gb_square[:], 0.0)
+        nc.scalar.copy(out=gb_square[0 : 2 * O_TILES, :], in_=gb_rows[:])
+        gb_bank = t_pool.tile([P, P], F32, tag="turned")
+        nc.tensor.transpose(gb_bank[:], gb_square[:], identity[:])
+        g_pair = keep.tile([P, O_TILES, 2], F32, name="g_pair")
+        b_col = keep.tile([P, O_TILES], F32, name="b_col")
+
+        grouped = {}
+        codes = {}
+        planes = {}
+        z = {}
+        stats = {}
+        gain = {}
+        shift = {}
+        y = {}
+        r = {}
+        turned = {}
+
+        def regroup(c):
+            grouped[c] = group_pool.tile([P, NODES, PACK], BF16, name="grouped", align_bytes=64)
+            src = raw[c // PASSES, c % PASSES][:].rearrange("p t (c i) -> p c t i", i=RUN)
+            dst = grouped[c][:].rearrange("p (c i) t -> p c t i", i=RUN)
+            nc.vector.tensor_copy(out=dst[:, :VECTOR_RUNS], in_=src[:, :VECTOR_RUNS])
+            nc.scalar.copy(out=dst[:, VECTOR_RUNS:], in_=src[:, VECTOR_RUNS:])
+
+        def quantise(c):
+            codes[c] = keep.tile([P, NODES], U32, name="codes_%d" % c, align_bytes=64)
+            planes[c] = keep.tile([P, NODES], U8, name="planes_%d" % c, align_bytes=64)
+            nc.vector.quantize_mx(
+                out=codes[c][:].bitcast(FP8X4),
+                scales=planes[c][:],
+                in_=grouped[c][:].rearrange("p n t -> p (n t)"),
+            )
+
+        def sums(i):
+            t, b = i // GRAPHS, i % GRAPHS
+            z[i] = z_pool.tile([P, NODES], F32, name="z")
+            for g in range(PASSES):
+                nc.tensor.matmul_mx(
+                    out=z[i][:],
+                    lhsT=w_words[:, g, 2 * P * t : 2 * P * (t + 1)].bitcast(FP4X4),
+                    lhsT_scale=w_planes[:, g, P * t : P * (t + 1)],
+                    rhs=codes[b * PASSES + g][:].bitcast(FP8X4),
+                    rhs_scale=planes[b * PASSES + g][:],
+                    start=(g == 0),
+                    stop=(g == PASSES - 1),
+                )
+
+        def statistics(i):
+            t, b = i // GRAPHS, i % GRAPHS
+            if b == 0:
+                stats[t] = small.tile([P, GRAPHS, 6], F32, name="stats")
+            nc.vector.bn_stats(out=stats[t][:, b, :], in_=z[i][:])
+
+        def gain_and_shift(t):
+            mean_var = small.tile([P, 2], F32, name="mean_var")
+            nc.vector.bn_aggr(out=mean_var[:], in_=stats[t][:].rearrange("p b s -> p (b s)"))
+            var_eps = small.tile([P, 1], F32, name="var_eps")
+            nc.gpsimd.tensor_scalar(out=var_eps[:], in0=mean_var[:, 1:2], scalar1=EPS_BN, scalar2=None, op0=ALU.add)
+            rstd = small.tile([P, 1], F32, name="rstd")
+            nc.gpsimd.tensor_tensor(out=rstd[:], in0=var_eps[:], in1=minus_half[:], op=ALU.pow)
+            gain[t] = small.tile([P, 2], F32, name="gain")
+            nc.gpsimd.tensor_scalar(out=gain[t][:], in0=g_pair[:, t, :], scalar1=rstd[:], scalar2=None, op0=ALU.mult)
+            shift[t] = small.tile([P, 1], F32, name="shift")
+            nc.gpsimd.tensor_scalar(
+                out=shift[t][:],
+                in0=mean_var[:, 0:1],
+                scalar1=gain[t][:, 1:2],
+                scalar2=b_col[:, t : t + 1],
+                op0=ALU.mult,
+                op1=ALU.add,
+            )
+
+        def normalise(i):
+            t = i // GRAPHS
+            y[i] = work.tile([P, NODES], F32, name="y")
+            nc.scalar.activation(out=y[i][:], in_=z[i][:], func=ACT.Identity, bias=shift[t][:], scale=gain[t][:, 0:1])
+
+        def leaky_relu(i):
+            r[i] = work.tile([P, NODES], F32, name="r")
+            nc.vector.scalar_tensor_tensor(
+                out=r[i][:], in0=y[i][:], scalar=NEG_SLOPE, in1=y[i][:], op0=ALU.mult, op1=ALU.max
+            )
+
+        def turn(i):
+            turned[i] = t_pool.tile([P, N_TILES, P], F32, tag="turned", name="turned")
+            for j in range(N_TILES):
+                nc.tensor.transpose(turned[i][:, j, :], r[i][:, j * P : (j + 1) * P], identity[:])
+
+        def store(i):
+            t, b = i // GRAPHS, i % GRAPHS
+            result = work.tile([P, N_TILES, P], F32, name="result")
+            nc.scalar.copy(out=result[:], in_=turned[i][:])
+            nc.sync.dma_start(
+                out=out[b].rearrange("(j p) o -> p j o", p=P)[:, :, t * P : (t + 1) * P],
+                in_=result[:],
+            )
+
+        chunks = GRAPHS * PASSES
+        for c in range(chunks + 1):
+            if c < chunks:
+                regroup(c)
+            if c >= 1:
+                quantise(c - 1)
+            if c >= PASSES + 1 and c % PASSES == 1:
+                statistics((c - 1) // PASSES - 1)
+            if c >= 1 and c % PASSES == 0:
+                sums(c // PASSES - 1)
+        nc.scalar.copy(out=g_pair[:, :, 0], in_=gb_bank[:, 0:O_TILES])
+        nc.scalar.mul(out=g_pair[:, :, 1], in_=gb_bank[:, 0:O_TILES], mul=-1.0)
+        nc.scalar.copy(out=b_col[:], in_=gb_bank[:, O_TILES : 2 * O_TILES])
+
+        for j in range(GRAPHS - 1, BANKS + LAG + 2):
+            k = j - LAG
+            if 0 <= k < BANKS:
+                normalise(k)
+            if j < BANKS:
+                statistics(j)
+                if j % GRAPHS == GRAPHS - 1:
+                    gain_and_shift(j // GRAPHS)
+            if 0 <= k < BANKS:
+                leaky_relu(k)
+            if j + 1 < BANKS:
+                sums(j + 1)
+            if 0 <= k - 1 < BANKS:
+                turn(k - 1)
+            if 0 <= k - 2 < BANKS:
+                store(k - 2)

@@ -21,7 +21,7 @@ GRAPHS, CHANNELS_IN, NODES, CHANNELS_OUT = 4, 1024, 512, 512
 PASSES = CHANNELS_IN // K_PASS
 O_TILES = CHANNELS_OUT // P
 N_TILES = NODES // P
-BANKS = O_TILES * GRAPHS
+UNITS = GRAPHS * O_TILES
 EPS_BN = 1e-5
 NEG_SLOPE = 0.01
 
@@ -29,8 +29,7 @@ FLOPS = 2 * GRAPHS * NODES * CHANNELS_IN * CHANNELS_OUT
 
 RUN = 4
 RUNS = NODES // RUN
-VECTOR_RUNS = 56
-LAG = 5
+VECTOR_RUNS = RUNS // 2
 
 
 def tile_yuyipointupdate_pb_kernel(tc, h1, W2_words, W2_scales, g2, b2, out):
@@ -38,10 +37,8 @@ def tile_yuyipointupdate_pb_kernel(tc, h1, W2_words, W2_scales, g2, b2, out):
     with ExitStack() as ctx:
         keep = ctx.enter_context(tc.tile_pool(name="keep", bufs=1))
         group_pool = ctx.enter_context(tc.tile_pool(name="group", bufs=3))
-        work = ctx.enter_context(tc.tile_pool(name="work", bufs=4))
-        small = ctx.enter_context(tc.tile_pool(name="small", bufs=2))
-        z_pool = ctx.enter_context(tc.psum_pool(name="z", bufs=LAG + 1))
-        t_pool = ctx.enter_context(tc.psum_pool(name="t", bufs=2))
+        work = ctx.enter_context(tc.tile_pool(name="work", bufs=2 * O_TILES))
+        psum = ctx.enter_context(tc.psum_pool(name="psum", bufs=8))
         ctx.enter_context(tc.manual_schedule())
 
         w_planes = keep.tile([P, PASSES, CHANNELS_OUT], U8, name="w_planes", align_bytes=64)
@@ -69,29 +66,23 @@ def tile_yuyipointupdate_pb_kernel(tc, h1, W2_words, W2_scales, g2, b2, out):
         for b in range(1, GRAPHS):
             load_graph(b)
 
-        minus_half = keep.tile([P, 1], F32, name="minus_half")
-        nc.gpsimd.memset(minus_half[:], -0.5)
+        eps = keep.tile([P, 1], F32, name="eps")
+        nc.vector.memset(eps[:], EPS_BN)
+        warm = keep.tile([P, 1], F32, name="warm")
+        nc.scalar.activation(out=warm[:], in_=eps[:], func=ACT.Sqrt)
         identity = keep.tile([P, P], F32, name="identity")
         masks.make_identity(nc, identity[:])
 
         gb_square = keep.tile([P, P], F32, name="gb_square")
         nc.vector.memset(gb_square[:], 0.0)
         nc.scalar.copy(out=gb_square[0 : 2 * O_TILES, :], in_=gb_rows[:])
-        gb_bank = t_pool.tile([P, P], F32, tag="turned")
+        gb_bank = psum.tile([P, P], F32, tag="bank", name="gb_bank")
         nc.tensor.transpose(gb_bank[:], gb_square[:], identity[:])
-        g_pair = keep.tile([P, O_TILES, 2], F32, name="g_pair")
-        b_col = keep.tile([P, O_TILES], F32, name="b_col")
+        gb = keep.tile([P, 2 * O_TILES], F32, name="gb")
 
         grouped = {}
         codes = {}
         planes = {}
-        z = {}
-        stats = {}
-        gain = {}
-        shift = {}
-        y = {}
-        r = {}
-        turned = {}
 
         def regroup(c):
             grouped[c] = group_pool.tile([P, NODES, PACK], BF16, name="grouped", align_bytes=64)
@@ -109,12 +100,23 @@ def tile_yuyipointupdate_pb_kernel(tc, h1, W2_words, W2_scales, g2, b2, out):
                 in_=grouped[c][:].rearrange("p n t -> p (n t)"),
             )
 
-        def sums(i):
-            t, b = i // GRAPHS, i % GRAPHS
-            z[i] = z_pool.tile([P, NODES], F32, name="z")
+        chunks = GRAPHS * PASSES
+        for c in range(chunks + 1):
+            if c < chunks:
+                regroup(c)
+            if c >= 1:
+                quantise(c - 1)
+        nc.scalar.copy(out=gb[:], in_=gb_bank[:, 0 : 2 * O_TILES])
+
+        z_sb = {}
+        stats = keep.tile([P, O_TILES, GRAPHS, 6], F32, name="stats")
+        mean_var = keep.tile([P, O_TILES, 2], F32, name="mean_var")
+        for i in range(UNITS):
+            b, t = i // O_TILES, i % O_TILES
+            z = psum.tile([P, NODES], F32, tag="bank", name="z")
             for g in range(PASSES):
                 nc.tensor.matmul_mx(
-                    out=z[i][:],
+                    out=z[:],
                     lhsT=w_words[:, g, 2 * P * t : 2 * P * (t + 1)].bitcast(FP4X4),
                     lhsT_scale=w_planes[:, g, P * t : P * (t + 1)],
                     rhs=codes[b * PASSES + g][:].bitcast(FP8X4),
@@ -122,84 +124,63 @@ def tile_yuyipointupdate_pb_kernel(tc, h1, W2_words, W2_scales, g2, b2, out):
                     start=(g == 0),
                     stop=(g == PASSES - 1),
                 )
+            z_sb[i] = keep.tile([P, NODES], F32, name="z_sb_%d" % i)
+            nc.scalar.copy(out=z_sb[i][:], in_=z[:])
+            nc.vector.bn_stats(out=stats[:, t, b, :], in_=z_sb[i][:])
+            if b == GRAPHS - 1:
+                nc.vector.bn_aggr(out=mean_var[:, t, :], in_=stats[:, t, :, :].rearrange("p b s -> p (b s)"))
 
-        def statistics(i):
-            t, b = i // GRAPHS, i % GRAPHS
-            if b == 0:
-                stats[t] = small.tile([P, GRAPHS, 6], F32, name="stats")
-            nc.vector.bn_stats(out=stats[t][:, b, :], in_=z[i][:])
+        std = keep.tile([P, O_TILES], F32, name="std")
+        nc.scalar.activation(out=std[:], in_=mean_var[:, :, 1], func=ACT.Sqrt, bias=eps[:])
+        rstd = keep.tile([P, O_TILES], F32, name="rstd")
+        nc.vector.reciprocal(out=rstd[:], in_=std[:])
+        gain = keep.tile([P, O_TILES], F32, name="gain")
+        nc.vector.tensor_mul(out=gain[:], in0=rstd[:], in1=gb[:, 0:O_TILES])
+        mean_gain = keep.tile([P, O_TILES], F32, name="mean_gain")
+        nc.vector.tensor_mul(out=mean_gain[:], in0=mean_var[:, :, 0], in1=gain[:])
+        shift = keep.tile([P, O_TILES], F32, name="shift")
+        nc.vector.tensor_sub(out=shift[:], in0=gb[:, O_TILES : 2 * O_TILES], in1=mean_gain[:])
 
-        def gain_and_shift(t):
-            mean_var = small.tile([P, 2], F32, name="mean_var")
-            nc.vector.bn_aggr(out=mean_var[:], in_=stats[t][:].rearrange("p b s -> p (b s)"))
-            var_eps = small.tile([P, 1], F32, name="var_eps")
-            nc.gpsimd.tensor_scalar(out=var_eps[:], in0=mean_var[:, 1:2], scalar1=EPS_BN, scalar2=None, op0=ALU.add)
-            rstd = small.tile([P, 1], F32, name="rstd")
-            nc.gpsimd.tensor_tensor(out=rstd[:], in0=var_eps[:], in1=minus_half[:], op=ALU.pow)
-            gain[t] = small.tile([P, 2], F32, name="gain")
-            nc.gpsimd.tensor_scalar(out=gain[t][:], in0=g_pair[:, t, :], scalar1=rstd[:], scalar2=None, op0=ALU.mult)
-            shift[t] = small.tile([P, 1], F32, name="shift")
-            nc.gpsimd.tensor_scalar(
-                out=shift[t][:],
-                in0=mean_var[:, 0:1],
-                scalar1=gain[t][:, 1:2],
-                scalar2=b_col[:, t : t + 1],
-                op0=ALU.mult,
-                op1=ALU.add,
-            )
+        y = {}
 
-        def normalise(i):
-            t = i // GRAPHS
-            y[i] = work.tile([P, NODES], F32, name="y")
-            nc.scalar.activation(out=y[i][:], in_=z[i][:], func=ACT.Identity, bias=shift[t][:], scale=gain[t][:, 0:1])
+        def normalise(b):
+            for t in range(O_TILES):
+                i = b * O_TILES + t
+                y[i] = work.tile([P, NODES], F32, name="y")
+                if t == 0:
+                    nc.scalar.activation(
+                        out=y[i][:], in_=z_sb[i][:], func=ACT.Identity, bias=shift[:, t : t + 1], scale=gain[:, t : t + 1]
+                    )
+                else:
+                    nc.vector.tensor_scalar(
+                        out=y[i][:],
+                        in0=z_sb[i][:],
+                        scalar1=gain[:, t : t + 1],
+                        scalar2=shift[:, t : t + 1],
+                        op0=ALU.mult,
+                        op1=ALU.add,
+                    )
 
-        def leaky_relu(i):
-            r[i] = work.tile([P, NODES], F32, name="r")
-            nc.vector.scalar_tensor_tensor(
-                out=r[i][:], in0=y[i][:], scalar=NEG_SLOPE, in1=y[i][:], op0=ALU.mult, op1=ALU.max
-            )
-
-        def turn(i):
-            turned[i] = t_pool.tile([P, N_TILES, P], F32, tag="turned", name="turned")
+        def finish(b):
+            turned = [psum.tile([P, CHANNELS_OUT], F32, tag="bank", name="turned_%d" % j) for j in range(N_TILES)]
+            for t in range(O_TILES):
+                i = b * O_TILES + t
+                r = work.tile([P, NODES], F32, name="r")
+                nc.vector.scalar_tensor_tensor(
+                    out=r[:], in0=y[i][:], scalar=NEG_SLOPE, in1=y[i][:], op0=ALU.mult, op1=ALU.max
+                )
+                for j in range(N_TILES):
+                    nc.tensor.transpose(turned[j][:, t * P : (t + 1) * P], r[:, j * P : (j + 1) * P], identity[:])
             for j in range(N_TILES):
-                nc.tensor.transpose(turned[i][:, j, :], r[i][:, j * P : (j + 1) * P], identity[:])
+                result = work.tile([P, CHANNELS_OUT], F32, name="result")
+                if b == GRAPHS - 1 and j % 2 == 1:
+                    nc.vector.tensor_copy(out=result[:], in_=turned[j][:])
+                else:
+                    nc.scalar.copy(out=result[:], in_=turned[j][:])
+                nc.sync.dma_start(out=out[b, j * P : (j + 1) * P, :], in_=result[:])
 
-        def store(i):
-            t, b = i // GRAPHS, i % GRAPHS
-            result = work.tile([P, N_TILES, P], F32, name="result")
-            nc.scalar.copy(out=result[:], in_=turned[i][:])
-            nc.sync.dma_start(
-                out=out[b].rearrange("(j p) o -> p j o", p=P)[:, :, t * P : (t + 1) * P],
-                in_=result[:],
-            )
-
-        chunks = GRAPHS * PASSES
-        for c in range(chunks + 1):
-            if c < chunks:
-                regroup(c)
-            if c >= 1:
-                quantise(c - 1)
-            if c >= PASSES + 1 and c % PASSES == 1:
-                statistics((c - 1) // PASSES - 1)
-            if c >= 1 and c % PASSES == 0:
-                sums(c // PASSES - 1)
-        nc.scalar.copy(out=g_pair[:, :, 0], in_=gb_bank[:, 0:O_TILES])
-        nc.scalar.mul(out=g_pair[:, :, 1], in_=gb_bank[:, 0:O_TILES], mul=-1.0)
-        nc.scalar.copy(out=b_col[:], in_=gb_bank[:, O_TILES : 2 * O_TILES])
-
-        for j in range(GRAPHS - 1, BANKS + LAG + 2):
-            k = j - LAG
-            if 0 <= k < BANKS:
-                normalise(k)
-            if j < BANKS:
-                statistics(j)
-                if j % GRAPHS == GRAPHS - 1:
-                    gain_and_shift(j // GRAPHS)
-            if 0 <= k < BANKS:
-                leaky_relu(k)
-            if j + 1 < BANKS:
-                sums(j + 1)
-            if 0 <= k - 1 < BANKS:
-                turn(k - 1)
-            if 0 <= k - 2 < BANKS:
-                store(k - 2)
+        normalise(0)
+        for b in range(GRAPHS):
+            if b + 1 < GRAPHS:
+                normalise(b + 1)
+            finish(b)

@@ -69,7 +69,7 @@ def tile_yuyipointupdate_pb_kernel(tc, h1, W2_words, W2_scales, g2, b2, out):
         eps = keep.tile([P, 1], F32, name="eps")
         nc.vector.memset(eps[:], EPS_BN)
         warm = keep.tile([P, 1], F32, name="warm")
-        nc.scalar.activation(out=warm[:], in_=eps[:], func=ACT.Sqrt)
+        nc.scalar.activation(out=warm[:], in_=eps[:], func=ACT.Abs_reciprocal_sqrt)
         identity = keep.tile([P, P], F32, name="identity")
         masks.make_identity(nc, identity[:])
 
@@ -130,10 +130,8 @@ def tile_yuyipointupdate_pb_kernel(tc, h1, W2_words, W2_scales, g2, b2, out):
             if b == GRAPHS - 1:
                 nc.vector.bn_aggr(out=mean_var[:, t, :], in_=stats[:, t, :, :].rearrange("p b s -> p (b s)"))
 
-        std = keep.tile([P, O_TILES], F32, name="std")
-        nc.scalar.activation(out=std[:], in_=mean_var[:, :, 1], func=ACT.Sqrt, bias=eps[:])
         rstd = keep.tile([P, O_TILES], F32, name="rstd")
-        nc.vector.reciprocal(out=rstd[:], in_=std[:])
+        nc.scalar.activation(out=rstd[:], in_=mean_var[:, :, 1], func=ACT.Abs_reciprocal_sqrt, bias=eps[:])
         gain = keep.tile([P, O_TILES], F32, name="gain")
         nc.vector.tensor_mul(out=gain[:], in0=rstd[:], in1=gb[:, 0:O_TILES])
         mean_gain = keep.tile([P, O_TILES], F32, name="mean_gain")
@@ -152,7 +150,8 @@ def tile_yuyipointupdate_pb_kernel(tc, h1, W2_words, W2_scales, g2, b2, out):
                         out=y[i][:], in_=z_sb[i][:], func=ACT.Identity, bias=shift[:, t : t + 1], scale=gain[:, t : t + 1]
                     )
                 else:
-                    nc.vector.tensor_scalar(
+                    engine = nc.vector if t == 1 else nc.gpsimd
+                    engine.tensor_scalar(
                         out=y[i][:],
                         in0=z_sb[i][:],
                         scalar1=gain[:, t : t + 1],
@@ -163,20 +162,16 @@ def tile_yuyipointupdate_pb_kernel(tc, h1, W2_words, W2_scales, g2, b2, out):
 
         def finish(b):
             turned = [psum.tile([P, CHANNELS_OUT], F32, tag="bank", name="turned_%d" % j) for j in range(N_TILES)]
-            for t in range(O_TILES):
-                i = b * O_TILES + t
-                r = work.tile([P, NODES], F32, name="r")
-                nc.vector.scalar_tensor_tensor(
-                    out=r[:], in0=y[i][:], scalar=NEG_SLOPE, in1=y[i][:], op0=ALU.mult, op1=ALU.max
-                )
-                for j in range(N_TILES):
-                    nc.tensor.transpose(turned[j][:, t * P : (t + 1) * P], r[:, j * P : (j + 1) * P], identity[:])
             for j in range(N_TILES):
+                for t in range(O_TILES):
+                    nc.tensor.transpose(
+                        turned[j][:, t * P : (t + 1) * P], y[b * O_TILES + t][:, j * P : (j + 1) * P], identity[:]
+                    )
+            for j in range(N_TILES):
+                sloped = work.tile([P, CHANNELS_OUT], F32, name="sloped")
+                nc.scalar.mul(out=sloped[:], in_=turned[j][:], mul=NEG_SLOPE)
                 result = work.tile([P, CHANNELS_OUT], F32, name="result")
-                if b == GRAPHS - 1 and j % 2 == 1:
-                    nc.vector.tensor_copy(out=result[:], in_=turned[j][:])
-                else:
-                    nc.scalar.copy(out=result[:], in_=turned[j][:])
+                nc.vector.tensor_tensor(out=result[:], in0=turned[j][:], in1=sloped[:], op=ALU.max)
                 nc.sync.dma_start(out=out[b, j * P : (j + 1) * P, :], in_=result[:])
 
         normalise(0)

@@ -29,7 +29,7 @@ FLOPS = 2 * GRAPHS * NODES * CHANNELS_IN * CHANNELS_OUT
 
 RUN = 4
 RUNS = NODES // RUN
-VECTOR_RUNS = RUNS // 2
+VECTOR_RUNS = 3 * RUNS // 8
 
 
 def tile_yuyipointupdate_pb_kernel(tc, h1, W2_words, W2_scales, g2, b2, out):
@@ -91,6 +91,17 @@ def tile_yuyipointupdate_pb_kernel(tc, h1, W2_words, W2_scales, g2, b2, out):
             nc.vector.tensor_copy(out=dst[:, :VECTOR_RUNS], in_=src[:, :VECTOR_RUNS])
             nc.scalar.copy(out=dst[:, VECTOR_RUNS:], in_=src[:, VECTOR_RUNS:])
 
+        def regroup_on_gpsimd(c):
+            grouped[c] = keep.tile([P, NODES, PACK], BF16, name="grouped_%d" % c, align_bytes=64)
+            nc.gpsimd.tensor_scalar(
+                out=grouped[c][:],
+                in0=raw[c // PASSES, c % PASSES][:].rearrange("p t n -> p n t"),
+                scalar1=1.0,
+                scalar2=0.0,
+                op0=ALU.mult,
+                op1=ALU.add,
+            )
+
         def quantise(c):
             codes[c] = keep.tile([P, NODES], U32, name="codes_%d" % c, align_bytes=64)
             planes[c] = keep.tile([P, NODES], U8, name="planes_%d" % c, align_bytes=64)
@@ -101,34 +112,53 @@ def tile_yuyipointupdate_pb_kernel(tc, h1, W2_words, W2_scales, g2, b2, out):
             )
 
         chunks = GRAPHS * PASSES
-        for c in range(chunks + 1):
-            if c < chunks:
+        shared = chunks - PASSES
+        for c in range(shared + 1):
+            if c < shared:
                 regroup(c)
             if c >= 1:
                 quantise(c - 1)
+        for c in range(shared, chunks):
+            regroup_on_gpsimd(c)
         nc.scalar.copy(out=gb[:], in_=gb_bank[:, 0 : 2 * O_TILES])
 
+        z = {}
         z_sb = {}
         stats = keep.tile([P, O_TILES, GRAPHS, 6], F32, name="stats")
         mean_var = keep.tile([P, O_TILES, 2], F32, name="mean_var")
-        for i in range(UNITS):
-            b, t = i // O_TILES, i % O_TILES
-            z = psum.tile([P, NODES], F32, tag="bank", name="z")
-            for g in range(PASSES):
-                nc.tensor.matmul_mx(
-                    out=z[:],
-                    lhsT=w_words[:, g, 2 * P * t : 2 * P * (t + 1)].bitcast(FP4X4),
-                    lhsT_scale=w_planes[:, g, P * t : P * (t + 1)],
-                    rhs=codes[b * PASSES + g][:].bitcast(FP8X4),
-                    rhs_scale=planes[b * PASSES + g][:],
-                    start=(g == 0),
-                    stop=(g == PASSES - 1),
-                )
-            z_sb[i] = keep.tile([P, NODES], F32, name="z_sb_%d" % i)
-            nc.scalar.copy(out=z_sb[i][:], in_=z[:])
-            nc.vector.bn_stats(out=stats[:, t, b, :], in_=z_sb[i][:])
-            if b == GRAPHS - 1:
-                nc.vector.bn_aggr(out=mean_var[:, t, :], in_=stats[:, t, :, :].rearrange("p b s -> p (b s)"))
+
+        def sums(b):
+            for t in range(O_TILES):
+                z[b, t] = psum.tile([P, NODES], F32, tag="bank", name="z")
+                for g in range(PASSES):
+                    nc.tensor.matmul_mx(
+                        out=z[b, t][:],
+                        lhsT=w_words[:, g, 2 * P * t : 2 * P * (t + 1)].bitcast(FP4X4),
+                        lhsT_scale=w_planes[:, g, P * t : P * (t + 1)],
+                        rhs=codes[b * PASSES + g][:].bitcast(FP8X4),
+                        rhs_scale=planes[b * PASSES + g][:],
+                        start=(g == 0),
+                        stop=(g == PASSES - 1),
+                    )
+
+        def statistics(b):
+            for t in range(O_TILES):
+                i = b * O_TILES + t
+                z_sb[i] = keep.tile([P, NODES], F32, name="z_sb_%d" % i)
+                nc.scalar.copy(out=z_sb[i][:], in_=z[b, t][:])
+                nc.vector.bn_stats(out=stats[:, t, b, :], in_=z_sb[i][:])
+                if b == GRAPHS - 1:
+                    nc.vector.bn_aggr(out=mean_var[:, t, :], in_=stats[:, t, :, :].rearrange("p b s -> p (b s)"))
+
+        sums(0)
+        sums(1)
+        for b in range(GRAPHS):
+            statistics(b)
+            if b + 2 == GRAPHS - 1:
+                for c in range(shared, chunks):
+                    quantise(c)
+            if b + 2 < GRAPHS:
+                sums(b + 2)
 
         rstd = keep.tile([P, O_TILES], F32, name="rstd")
         nc.scalar.activation(out=rstd[:], in_=mean_var[:, :, 1], func=ACT.Abs_reciprocal_sqrt, bias=eps[:])
@@ -145,7 +175,7 @@ def tile_yuyipointupdate_pb_kernel(tc, h1, W2_words, W2_scales, g2, b2, out):
             for t in range(O_TILES):
                 i = b * O_TILES + t
                 y[i] = work.tile([P, NODES], F32, name="y")
-                if t == 0:
+                if t == 0 and b == 0:
                     nc.scalar.activation(
                         out=y[i][:], in_=z_sb[i][:], func=ACT.Identity, bias=shift[:, t : t + 1], scale=gain[:, t : t + 1]
                     )

@@ -29,7 +29,7 @@ FLOPS = 2 * GRAPHS * NODES * CHANNELS_IN * CHANNELS_OUT
 
 RUN = 4
 RUNS = NODES // RUN
-VECTOR_RUNS = 3 * RUNS // 8
+VECTOR_RUNS = RUNS // 2
 
 
 def tile_yuyipointupdate_pb_kernel(tc, h1, W2_words, W2_scales, g2, b2, out):
@@ -91,17 +91,6 @@ def tile_yuyipointupdate_pb_kernel(tc, h1, W2_words, W2_scales, g2, b2, out):
             nc.vector.tensor_copy(out=dst[:, :VECTOR_RUNS], in_=src[:, :VECTOR_RUNS])
             nc.scalar.copy(out=dst[:, VECTOR_RUNS:], in_=src[:, VECTOR_RUNS:])
 
-        def regroup_on_gpsimd(c):
-            grouped[c] = keep.tile([P, NODES, PACK], BF16, name="grouped_%d" % c, align_bytes=64)
-            nc.gpsimd.tensor_scalar(
-                out=grouped[c][:],
-                in0=raw[c // PASSES, c % PASSES][:].rearrange("p t n -> p n t"),
-                scalar1=1.0,
-                scalar2=0.0,
-                op0=ALU.mult,
-                op1=ALU.add,
-            )
-
         def quantise(c):
             codes[c] = keep.tile([P, NODES], U32, name="codes_%d" % c, align_bytes=64)
             planes[c] = keep.tile([P, NODES], U8, name="planes_%d" % c, align_bytes=64)
@@ -112,53 +101,34 @@ def tile_yuyipointupdate_pb_kernel(tc, h1, W2_words, W2_scales, g2, b2, out):
             )
 
         chunks = GRAPHS * PASSES
-        shared = chunks - PASSES
-        for c in range(shared + 1):
-            if c < shared:
+        for c in range(chunks + 1):
+            if c < chunks:
                 regroup(c)
             if c >= 1:
                 quantise(c - 1)
-        for c in range(shared, chunks):
-            regroup_on_gpsimd(c)
         nc.scalar.copy(out=gb[:], in_=gb_bank[:, 0 : 2 * O_TILES])
 
-        z = {}
         z_sb = {}
         stats = keep.tile([P, O_TILES, GRAPHS, 6], F32, name="stats")
         mean_var = keep.tile([P, O_TILES, 2], F32, name="mean_var")
-
-        def sums(b):
-            for t in range(O_TILES):
-                z[b, t] = psum.tile([P, NODES], F32, tag="bank", name="z")
-                for g in range(PASSES):
-                    nc.tensor.matmul_mx(
-                        out=z[b, t][:],
-                        lhsT=w_words[:, g, 2 * P * t : 2 * P * (t + 1)].bitcast(FP4X4),
-                        lhsT_scale=w_planes[:, g, P * t : P * (t + 1)],
-                        rhs=codes[b * PASSES + g][:].bitcast(FP8X4),
-                        rhs_scale=planes[b * PASSES + g][:],
-                        start=(g == 0),
-                        stop=(g == PASSES - 1),
-                    )
-
-        def statistics(b):
-            for t in range(O_TILES):
-                i = b * O_TILES + t
-                z_sb[i] = keep.tile([P, NODES], F32, name="z_sb_%d" % i)
-                nc.scalar.copy(out=z_sb[i][:], in_=z[b, t][:])
-                nc.vector.bn_stats(out=stats[:, t, b, :], in_=z_sb[i][:])
-                if b == GRAPHS - 1:
-                    nc.vector.bn_aggr(out=mean_var[:, t, :], in_=stats[:, t, :, :].rearrange("p b s -> p (b s)"))
-
-        sums(0)
-        sums(1)
-        for b in range(GRAPHS):
-            statistics(b)
-            if b + 2 == GRAPHS - 1:
-                for c in range(shared, chunks):
-                    quantise(c)
-            if b + 2 < GRAPHS:
-                sums(b + 2)
+        for i in range(UNITS):
+            b, t = i // O_TILES, i % O_TILES
+            z = psum.tile([P, NODES], F32, tag="bank", name="z")
+            for g in range(PASSES):
+                nc.tensor.matmul_mx(
+                    out=z[:],
+                    lhsT=w_words[:, g, 2 * P * t : 2 * P * (t + 1)].bitcast(FP4X4),
+                    lhsT_scale=w_planes[:, g, P * t : P * (t + 1)],
+                    rhs=codes[b * PASSES + g][:].bitcast(FP8X4),
+                    rhs_scale=planes[b * PASSES + g][:],
+                    start=(g == 0),
+                    stop=(g == PASSES - 1),
+                )
+            z_sb[i] = keep.tile([P, NODES], F32, name="z_sb_%d" % i)
+            nc.scalar.copy(out=z_sb[i][:], in_=z[:])
+            nc.vector.bn_stats(out=stats[:, t, b, :], in_=z_sb[i][:])
+            if b == GRAPHS - 1:
+                nc.vector.bn_aggr(out=mean_var[:, t, :], in_=stats[:, t, :, :].rearrange("p b s -> p (b s)"))
 
         rstd = keep.tile([P, O_TILES], F32, name="rstd")
         nc.scalar.activation(out=rstd[:], in_=mean_var[:, :, 1], func=ACT.Abs_reciprocal_sqrt, bias=eps[:])
@@ -172,15 +142,16 @@ def tile_yuyipointupdate_pb_kernel(tc, h1, W2_words, W2_scales, g2, b2, out):
         y = {}
 
         def normalise(b):
+            vector_tiles = 2 if b == 0 else 1
             for t in range(O_TILES):
                 i = b * O_TILES + t
                 y[i] = work.tile([P, NODES], F32, name="y")
-                if t == 0 and b == 0:
+                if t == 0:
                     nc.scalar.activation(
                         out=y[i][:], in_=z_sb[i][:], func=ACT.Identity, bias=shift[:, t : t + 1], scale=gain[:, t : t + 1]
                     )
                 else:
-                    engine = nc.vector if t == 1 else nc.gpsimd
+                    engine = nc.vector if t <= vector_tiles else nc.gpsimd
                     engine.tensor_scalar(
                         out=y[i][:],
                         in0=z_sb[i][:],

@@ -28,8 +28,12 @@ NEG_SLOPE = 0.01
 FLOPS = 2 * GRAPHS * NODES * CHANNELS_IN * CHANNELS_OUT
 
 RUN = 4
-RUNS = NODES // RUN
-VECTOR_RUNS = RUNS // 2
+TENSOR_NODES = 192
+VECTOR_NODES = NODES - TENSOR_NODES
+VECTOR_RUNS = VECTOR_NODES // RUN
+SCALAR_GRAPHS = 2
+TRIPLE = 3
+STATS_WIDTH = SCALAR_GRAPHS * TRIPLE + (GRAPHS - SCALAR_GRAPHS) * 2 * TRIPLE
 
 
 def tile_yuyipointupdate_pb_kernel(tc, h1, W2_words, W2_scales, g2, b2, out):
@@ -37,9 +41,12 @@ def tile_yuyipointupdate_pb_kernel(tc, h1, W2_words, W2_scales, g2, b2, out):
     with ExitStack() as ctx:
         keep = ctx.enter_context(tc.tile_pool(name="keep", bufs=1))
         group_pool = ctx.enter_context(tc.tile_pool(name="group", bufs=3))
-        work = ctx.enter_context(tc.tile_pool(name="work", bufs=2 * O_TILES))
-        psum = ctx.enter_context(tc.psum_pool(name="psum", bufs=8))
+        work = ctx.enter_context(tc.tile_pool(name="work", bufs=8))
+        psum = ctx.enter_context(tc.psum_pool(name="psum", bufs=1))
         ctx.enter_context(tc.manual_schedule())
+
+        def bank(k, shape, dtype, name):
+            return psum.tile(shape, dtype, tag="bank%d" % k, name=name)
 
         w_planes = keep.tile([P, PASSES, CHANNELS_OUT], U8, name="w_planes", align_bytes=64)
         nc.vector.memset(w_planes[:].bitcast(I32), 0)
@@ -56,9 +63,10 @@ def tile_yuyipointupdate_pb_kernel(tc, h1, W2_words, W2_scales, g2, b2, out):
 
         def load_graph(b):
             for g in range(PASSES):
-                raw[b, g] = keep.tile([P, PACK, NODES], BF16, name="raw_%d_%d" % (b, g))
+                c = b * PASSES + g
+                raw[c] = keep.tile([P, PACK, NODES], BF16, name="raw_%d" % c)
                 rows = h1[b, g * K_PASS : (g + 1) * K_PASS, :]
-                nc.sync.dma_start(out=raw[b, g][:], in_=rows.rearrange("(p t) n -> p t n", t=PACK))
+                nc.sync.dma_start(out=raw[c][:], in_=rows.rearrange("(p t) n -> p t n", t=PACK))
 
         load_graph(0)
         w_words = keep.tile([P, PASSES, 2 * CHANNELS_OUT], U8, name="w_words", align_bytes=64)
@@ -70,26 +78,47 @@ def tile_yuyipointupdate_pb_kernel(tc, h1, W2_words, W2_scales, g2, b2, out):
         nc.vector.memset(eps[:], EPS_BN)
         warm = keep.tile([P, 1], F32, name="warm")
         nc.scalar.activation(out=warm[:], in_=eps[:], func=ACT.Abs_reciprocal_sqrt)
+        identity_bf = keep.tile([P, P], BF16, name="identity_bf")
+        masks.make_identity(nc, identity_bf[:])
         identity = keep.tile([P, P], F32, name="identity")
         masks.make_identity(nc, identity[:])
-
         gb_square = keep.tile([P, P], F32, name="gb_square")
         nc.vector.memset(gb_square[:], 0.0)
-        nc.scalar.copy(out=gb_square[0 : 2 * O_TILES, :], in_=gb_rows[:])
-        gb_bank = psum.tile([P, P], F32, tag="bank", name="gb_bank")
-        nc.tensor.transpose(gb_bank[:], gb_square[:], identity[:])
         gb = keep.tile([P, 2 * O_TILES], F32, name="gb")
 
+        stats = keep.tile([P, O_TILES, STATS_WIDTH], F32, name="stats")
+        scalar_triples = stats[:, :, 0 : SCALAR_GRAPHS * TRIPLE].rearrange("p t (b s) -> p t b s", s=TRIPLE)
+        nc.vector.memset(scalar_triples[:, :, :, 0:1], float(NODES))
+        sums = keep.tile([P, SCALAR_GRAPHS, O_TILES], F32, name="sums")
+        mean_var = keep.tile([P, O_TILES, 2], F32, name="mean_var")
+
         grouped = {}
+        turned_in = {}
         codes = {}
         planes = {}
+        z = {}
+        z_sb = {}
+        y = {}
 
-        def regroup(c):
+        def regroup_tensor(c):
+            turned_in[c] = bank(6 + c % 2, [P, 2 * NODES], BF16, "turned_in")
+            src = raw[c][:, :, VECTOR_NODES:].rearrange("p t n -> p n t")
+            dst = turned_in[c][:, 0 : TENSOR_NODES * PACK].rearrange("p (n t) -> p n t", t=PACK)
+            for n0 in range(0, TENSOR_NODES, P):
+                n1 = min(n0 + P, TENSOR_NODES)
+                nc.tensor.matmul(out=dst[:, n0:n1, :], lhsT=identity_bf[:], rhs=src[:, n0:n1, :], start=True, stop=True)
+
+        def regroup_vector(c):
             grouped[c] = group_pool.tile([P, NODES, PACK], BF16, name="grouped", align_bytes=64)
-            src = raw[c // PASSES, c % PASSES][:].rearrange("p t (c i) -> p c t i", i=RUN)
+            src = raw[c][:].rearrange("p t (c i) -> p c t i", i=RUN)
             dst = grouped[c][:].rearrange("p (c i) t -> p c t i", i=RUN)
             nc.vector.tensor_copy(out=dst[:, :VECTOR_RUNS], in_=src[:, :VECTOR_RUNS])
-            nc.scalar.copy(out=dst[:, VECTOR_RUNS:], in_=src[:, VECTOR_RUNS:])
+
+        def regroup_scalar(c):
+            nc.scalar.copy(
+                out=grouped[c][:, VECTOR_NODES:, :].rearrange("p n t -> p (n t)"),
+                in_=turned_in[c][:, 0 : TENSOR_NODES * PACK],
+            )
 
         def quantise(c):
             codes[c] = keep.tile([P, NODES], U32, name="codes_%d" % c, align_bytes=64)
@@ -100,23 +129,11 @@ def tile_yuyipointupdate_pb_kernel(tc, h1, W2_words, W2_scales, g2, b2, out):
                 in_=grouped[c][:].rearrange("p n t -> p (n t)"),
             )
 
-        chunks = GRAPHS * PASSES
-        for c in range(chunks + 1):
-            if c < chunks:
-                regroup(c)
-            if c >= 1:
-                quantise(c - 1)
-        nc.scalar.copy(out=gb[:], in_=gb_bank[:, 0 : 2 * O_TILES])
-
-        z_sb = {}
-        stats = keep.tile([P, O_TILES, GRAPHS, 6], F32, name="stats")
-        mean_var = keep.tile([P, O_TILES, 2], F32, name="mean_var")
-        for i in range(UNITS):
-            b, t = i // O_TILES, i % O_TILES
-            z = psum.tile([P, NODES], F32, tag="bank", name="z")
+        def multiply(b, t, k):
+            z[b, t] = bank(k, [P, NODES], F32, "z")
             for g in range(PASSES):
                 nc.tensor.matmul_mx(
-                    out=z[:],
+                    out=z[b, t][:],
                     lhsT=w_words[:, g, 2 * P * t : 2 * P * (t + 1)].bitcast(FP4X4),
                     lhsT_scale=w_planes[:, g, P * t : P * (t + 1)],
                     rhs=codes[b * PASSES + g][:].bitcast(FP8X4),
@@ -124,11 +141,103 @@ def tile_yuyipointupdate_pb_kernel(tc, h1, W2_words, W2_scales, g2, b2, out):
                     start=(g == 0),
                     stop=(g == PASSES - 1),
                 )
-            z_sb[i] = keep.tile([P, NODES], F32, name="z_sb_%d" % i)
-            nc.scalar.copy(out=z_sb[i][:], in_=z[:])
-            nc.vector.bn_stats(out=stats[:, t, b, :], in_=z_sb[i][:])
-            if b == GRAPHS - 1:
-                nc.vector.bn_aggr(out=mean_var[:, t, :], in_=stats[:, t, :, :].rearrange("p b s -> p (b s)"))
+
+        def move_out(b, t):
+            z_sb[b, t] = keep.tile([P, NODES], F32, name="z_sb_%d_%d" % (b, t))
+            nc.scalar.activation(out=z_sb[b, t][:], in_=z[b, t][:], func=ACT.Copy, accum_out=sums[:, b, t : t + 1])
+
+        def means(b):
+            nc.scalar.mul(out=scalar_triples[:, :, b, 1], in_=sums[:, b, :], mul=1.0 / NODES)
+
+        def squares(b, t):
+            junk = work.tile([P, NODES], F32, name="junk")
+            nc.scalar.activation(
+                out=junk[:],
+                in_=z_sb[b, t][:],
+                func=ACT.Square,
+                scale=-1.0,
+                bias=scalar_triples[:, t, b, 1:2],
+                accum_out=scalar_triples[:, t, b, 2:3],
+            )
+
+        def measure(b, t):
+            first = SCALAR_GRAPHS * TRIPLE + (b - SCALAR_GRAPHS) * 2 * TRIPLE
+            nc.vector.bn_stats(out=stats[:, t, first : first + 2 * TRIPLE], in_=z[b, t][:])
+
+        regroup_tensor(0)
+        regroup_vector(0)
+        regroup_scalar(0)
+
+        regroup_tensor(1)
+        regroup_vector(1)
+        regroup_scalar(1)
+        quantise(0)
+        nc.scalar.copy(out=gb_square[0 : 2 * O_TILES, :], in_=gb_rows[:])
+
+        regroup_tensor(2)
+        gb_bank = bank(5, [P, P], F32, "gb_bank")
+        nc.tensor.transpose(gb_bank[:], gb_square[:], identity[:])
+        regroup_vector(2)
+        regroup_scalar(2)
+        quantise(1)
+
+        regroup_tensor(3)
+        for t in range(O_TILES):
+            multiply(0, t, t)
+        regroup_vector(3)
+        regroup_scalar(3)
+        quantise(2)
+        nc.scalar.copy(out=gb[:], in_=gb_bank[:, 0 : 2 * O_TILES])
+        move_out(0, 0)
+        move_out(0, 1)
+
+        regroup_tensor(4)
+        regroup_vector(4)
+        regroup_scalar(4)
+        quantise(3)
+        move_out(0, 2)
+        move_out(0, 3)
+        means(0)
+
+        regroup_tensor(5)
+        for t, k in enumerate((4, 5, 0, 1)):
+            multiply(1, t, k)
+        regroup_vector(5)
+        regroup_scalar(5)
+        quantise(4)
+        squares(0, 0)
+        squares(0, 1)
+
+        regroup_tensor(6)
+        regroup_vector(6)
+        regroup_scalar(6)
+        quantise(5)
+
+        regroup_tensor(7)
+        multiply(2, 0, 2)
+        multiply(2, 1, 3)
+        regroup_vector(7)
+        regroup_scalar(7)
+        quantise(6)
+        quantise(7)
+
+        move_out(1, 0)
+        move_out(1, 1)
+        multiply(2, 2, 4)
+        multiply(2, 3, 5)
+        move_out(1, 2)
+        move_out(1, 3)
+        for t, k in enumerate((6, 7, 0, 1)):
+            multiply(3, t, k)
+        means(1)
+        squares(0, 2)
+        squares(0, 3)
+        for t in range(O_TILES):
+            measure(2, t)
+            squares(1, t)
+        for t in range(O_TILES):
+            measure(3, t)
+            nc.vector.bn_aggr(out=mean_var[:, t, :], in_=stats[:, t, :])
 
         rstd = keep.tile([P, O_TILES], F32, name="rstd")
         nc.scalar.activation(out=rstd[:], in_=mean_var[:, :, 1], func=ACT.Abs_reciprocal_sqrt, bias=eps[:])
@@ -139,44 +248,55 @@ def tile_yuyipointupdate_pb_kernel(tc, h1, W2_words, W2_scales, g2, b2, out):
         shift = keep.tile([P, O_TILES], F32, name="shift")
         nc.vector.tensor_sub(out=shift[:], in0=gb[:, O_TILES : 2 * O_TILES], in1=mean_gain[:])
 
-        y = {}
-
         def normalise(b):
-            vector_tiles = 2 if b == 0 else 1
             for t in range(O_TILES):
-                i = b * O_TILES + t
-                y[i] = work.tile([P, NODES], F32, name="y")
-                if t == 0:
+                y[b, t] = keep.tile([P, NODES], F32, name="y_%d_%d" % (b, t))
+                if b < SCALAR_GRAPHS:
+                    nc.gpsimd.tensor_scalar(
+                        out=y[b, t][:],
+                        in0=z_sb[b, t][:],
+                        scalar1=gain[:, t : t + 1],
+                        scalar2=shift[:, t : t + 1],
+                        op0=ALU.mult,
+                        op1=ALU.add,
+                    )
+                elif t % 2 == 0:
                     nc.scalar.activation(
-                        out=y[i][:], in_=z_sb[i][:], func=ACT.Identity, bias=shift[:, t : t + 1], scale=gain[:, t : t + 1]
+                        out=y[b, t][:], in_=z[b, t][:], func=ACT.Identity, bias=shift[:, t : t + 1], scale=gain[:, t : t + 1]
                     )
                 else:
-                    engine = nc.vector if t <= vector_tiles else nc.gpsimd
-                    engine.tensor_scalar(
-                        out=y[i][:],
-                        in0=z_sb[i][:],
+                    nc.vector.tensor_scalar(
+                        out=y[b, t][:],
+                        in0=z[b, t][:],
                         scalar1=gain[:, t : t + 1],
                         scalar2=shift[:, t : t + 1],
                         op0=ALU.mult,
                         op1=ALU.add,
                     )
 
-        def finish(b):
-            turned = [psum.tile([P, CHANNELS_OUT], F32, tag="bank", name="turned_%d" % j) for j in range(N_TILES)]
+        def finish(b, banks, last=False):
+            turned = [bank(banks[j], [P, CHANNELS_OUT], F32, "turned_%d" % j) for j in range(N_TILES)]
             for j in range(N_TILES):
                 for t in range(O_TILES):
-                    nc.tensor.transpose(
-                        turned[j][:, t * P : (t + 1) * P], y[b * O_TILES + t][:, j * P : (j + 1) * P], identity[:]
-                    )
+                    nc.tensor.transpose(turned[j][:, t * P : (t + 1) * P], y[b, t][:, j * P : (j + 1) * P], identity[:])
             for j in range(N_TILES):
                 sloped = work.tile([P, CHANNELS_OUT], F32, name="sloped")
-                nc.scalar.mul(out=sloped[:], in_=turned[j][:], mul=NEG_SLOPE)
                 result = work.tile([P, CHANNELS_OUT], F32, name="result")
-                nc.vector.tensor_tensor(out=result[:], in0=turned[j][:], in1=sloped[:], op=ALU.max)
-                nc.sync.dma_start(out=out[b, j * P : (j + 1) * P, :], in_=result[:])
+                pieces = 2 if last and j == N_TILES - 1 else 1
+                width = CHANNELS_OUT // pieces
+                for o in range(0, CHANNELS_OUT, width):
+                    nc.scalar.mul(out=sloped[:, o : o + width], in_=turned[j][:, o : o + width], mul=NEG_SLOPE)
+                for o in range(0, CHANNELS_OUT, width):
+                    nc.vector.tensor_tensor(
+                        out=result[:, o : o + width], in0=turned[j][:, o : o + width], in1=sloped[:, o : o + width], op=ALU.max
+                    )
+                    nc.sync.dma_start(out=out[b, j * P : (j + 1) * P, o : o + width], in_=result[:, o : o + width])
 
+        normalise(2)
+        normalise(3)
         normalise(0)
-        for b in range(GRAPHS):
-            if b + 1 < GRAPHS:
-                normalise(b + 1)
-            finish(b)
+        normalise(1)
+        finish(2, (2, 3, 4, 5))
+        finish(3, (6, 7, 0, 1))
+        finish(0, (2, 3, 4, 5))
+        finish(1, (6, 7, 0, 1), last=True)

@@ -28,8 +28,7 @@ NEG_SLOPE = 0.01
 FLOPS = 2 * GRAPHS * NODES * CHANNELS_IN * CHANNELS_OUT
 
 RUN = 4
-TENSOR_NODES = 192
-VECTOR_NODES = NODES - TENSOR_NODES
+VECTOR_NODES = 320
 VECTOR_RUNS = VECTOR_NODES // RUN
 SCALAR_GRAPHS = 2
 TRIPLE = 3
@@ -78,8 +77,6 @@ def tile_yuyipointupdate_pb_kernel(tc, h1, W2_words, W2_scales, g2, b2, out):
         nc.vector.memset(eps[:], EPS_BN)
         warm = keep.tile([P, 1], F32, name="warm")
         nc.scalar.activation(out=warm[:], in_=eps[:], func=ACT.Abs_reciprocal_sqrt)
-        identity_bf = keep.tile([P, P], BF16, name="identity_bf")
-        masks.make_identity(nc, identity_bf[:])
         identity = keep.tile([P, P], F32, name="identity")
         masks.make_identity(nc, identity[:])
         gb_square = keep.tile([P, P], F32, name="gb_square")
@@ -93,20 +90,11 @@ def tile_yuyipointupdate_pb_kernel(tc, h1, W2_words, W2_scales, g2, b2, out):
         mean_var = keep.tile([P, O_TILES, 2], F32, name="mean_var")
 
         grouped = {}
-        turned_in = {}
         codes = {}
         planes = {}
         z = {}
         z_sb = {}
         y = {}
-
-        def regroup_tensor(c):
-            turned_in[c] = bank(6 + c % 2, [P, 2 * NODES], BF16, "turned_in")
-            src = raw[c][:, :, VECTOR_NODES:].rearrange("p t n -> p n t")
-            dst = turned_in[c][:, 0 : TENSOR_NODES * PACK].rearrange("p (n t) -> p n t", t=PACK)
-            for n0 in range(0, TENSOR_NODES, P):
-                n1 = min(n0 + P, TENSOR_NODES)
-                nc.tensor.matmul(out=dst[:, n0:n1, :], lhsT=identity_bf[:], rhs=src[:, n0:n1, :], start=True, stop=True)
 
         def regroup_vector(c):
             grouped[c] = group_pool.tile([P, NODES, PACK], BF16, name="grouped", align_bytes=64)
@@ -115,10 +103,9 @@ def tile_yuyipointupdate_pb_kernel(tc, h1, W2_words, W2_scales, g2, b2, out):
             nc.vector.tensor_copy(out=dst[:, :VECTOR_RUNS], in_=src[:, :VECTOR_RUNS])
 
         def regroup_scalar(c):
-            nc.scalar.copy(
-                out=grouped[c][:, VECTOR_NODES:, :].rearrange("p n t -> p (n t)"),
-                in_=turned_in[c][:, 0 : TENSOR_NODES * PACK],
-            )
+            src = raw[c][:].rearrange("p t (c i) -> p c t i", i=RUN)
+            dst = grouped[c][:].rearrange("p (c i) t -> p c t i", i=RUN)
+            nc.scalar.copy(out=dst[:, VECTOR_RUNS:], in_=src[:, VECTOR_RUNS:])
 
         def quantise(c):
             codes[c] = keep.tile([P, NODES], U32, name="codes_%d" % c, align_bytes=64)
@@ -164,24 +151,20 @@ def tile_yuyipointupdate_pb_kernel(tc, h1, W2_words, W2_scales, g2, b2, out):
             first = SCALAR_GRAPHS * TRIPLE + (b - SCALAR_GRAPHS) * 2 * TRIPLE
             nc.vector.bn_stats(out=stats[:, t, first : first + 2 * TRIPLE], in_=z[b, t][:])
 
-        regroup_tensor(0)
         regroup_vector(0)
         regroup_scalar(0)
 
-        regroup_tensor(1)
         regroup_vector(1)
         regroup_scalar(1)
         quantise(0)
         nc.scalar.copy(out=gb_square[0 : 2 * O_TILES, :], in_=gb_rows[:])
 
-        regroup_tensor(2)
         gb_bank = bank(5, [P, P], F32, "gb_bank")
         nc.tensor.transpose(gb_bank[:], gb_square[:], identity[:])
         regroup_vector(2)
         regroup_scalar(2)
         quantise(1)
 
-        regroup_tensor(3)
         for t in range(O_TILES):
             multiply(0, t, t)
         regroup_vector(3)
@@ -191,7 +174,6 @@ def tile_yuyipointupdate_pb_kernel(tc, h1, W2_words, W2_scales, g2, b2, out):
         move_out(0, 0)
         move_out(0, 1)
 
-        regroup_tensor(4)
         regroup_vector(4)
         regroup_scalar(4)
         quantise(3)
@@ -199,7 +181,6 @@ def tile_yuyipointupdate_pb_kernel(tc, h1, W2_words, W2_scales, g2, b2, out):
         move_out(0, 3)
         means(0)
 
-        regroup_tensor(5)
         for t, k in enumerate((4, 5, 0, 1)):
             multiply(1, t, k)
         regroup_vector(5)
@@ -208,12 +189,10 @@ def tile_yuyipointupdate_pb_kernel(tc, h1, W2_words, W2_scales, g2, b2, out):
         squares(0, 0)
         squares(0, 1)
 
-        regroup_tensor(6)
         regroup_vector(6)
         regroup_scalar(6)
         quantise(5)
 
-        regroup_tensor(7)
         multiply(2, 0, 2)
         multiply(2, 1, 3)
         regroup_vector(7)

@@ -28,8 +28,9 @@ NEG_SLOPE = 0.01
 FLOPS = 2 * GRAPHS * NODES * CHANNELS_IN * CHANNELS_OUT
 
 RUN = 4
-VECTOR_NODES = 320
-VECTOR_RUNS = VECTOR_NODES // RUN
+VECTOR_RUNS_EARLY = 76
+VECTOR_RUNS_LATE = 100
+EARLY_CHUNKS = 4
 SCALAR_GRAPHS = 2
 TRIPLE = 3
 STATS_WIDTH = SCALAR_GRAPHS * TRIPLE + (GRAPHS - SCALAR_GRAPHS) * 2 * TRIPLE
@@ -60,18 +61,14 @@ def tile_yuyipointupdate_pb_kernel(tc, h1, W2_words, W2_scales, g2, b2, out):
 
         raw = {}
 
-        def load_graph(b):
-            for g in range(PASSES):
-                c = b * PASSES + g
-                raw[c] = keep.tile([P, PACK, NODES], BF16, name="raw_%d" % c)
-                rows = h1[b, g * K_PASS : (g + 1) * K_PASS, :]
-                nc.sync.dma_start(out=raw[c][:], in_=rows.rearrange("(p t) n -> p t n", t=PACK))
-
-        load_graph(0)
         w_words = keep.tile([P, PASSES, 2 * CHANNELS_OUT], U8, name="w_words", align_bytes=64)
-        nc.sync.dma_start(out=w_words[:].bitcast(I32), in_=W2_words.bitcast(I32).rearrange("g p m -> p g m"))
-        for b in range(1, GRAPHS):
-            load_graph(b)
+        for c in range(GRAPHS * PASSES):
+            b, g = c // PASSES, c % PASSES
+            raw[c] = keep.tile([P, PACK, NODES], BF16, name="raw_%d" % c)
+            rows = h1[b, g * K_PASS : (g + 1) * K_PASS, :]
+            nc.sync.dma_start(out=raw[c][:], in_=rows.rearrange("(p t) n -> p t n", t=PACK))
+            if c == PASSES:
+                nc.sync.dma_start(out=w_words[:].bitcast(I32), in_=W2_words.bitcast(I32).rearrange("g p m -> p g m"))
 
         eps = keep.tile([P, 1], F32, name="eps")
         nc.vector.memset(eps[:], EPS_BN)
@@ -96,16 +93,19 @@ def tile_yuyipointupdate_pb_kernel(tc, h1, W2_words, W2_scales, g2, b2, out):
         z_sb = {}
         y = {}
 
+        def vector_runs(c):
+            return VECTOR_RUNS_EARLY if c < EARLY_CHUNKS else VECTOR_RUNS_LATE
+
         def regroup_vector(c):
             grouped[c] = group_pool.tile([P, NODES, PACK], BF16, name="grouped", align_bytes=64)
             src = raw[c][:].rearrange("p t (c i) -> p c t i", i=RUN)
             dst = grouped[c][:].rearrange("p (c i) t -> p c t i", i=RUN)
-            nc.vector.tensor_copy(out=dst[:, :VECTOR_RUNS], in_=src[:, :VECTOR_RUNS])
+            nc.vector.tensor_copy(out=dst[:, : vector_runs(c)], in_=src[:, : vector_runs(c)])
 
         def regroup_scalar(c):
             src = raw[c][:].rearrange("p t (c i) -> p c t i", i=RUN)
             dst = grouped[c][:].rearrange("p (c i) t -> p c t i", i=RUN)
-            nc.scalar.copy(out=dst[:, VECTOR_RUNS:], in_=src[:, VECTOR_RUNS:])
+            nc.scalar.copy(out=dst[:, vector_runs(c) :], in_=src[:, vector_runs(c) :])
 
         def quantise(c):
             codes[c] = keep.tile([P, NODES], U32, name="codes_%d" % c, align_bytes=64)
@@ -133,6 +133,10 @@ def tile_yuyipointupdate_pb_kernel(tc, h1, W2_words, W2_scales, g2, b2, out):
             z_sb[b, t] = keep.tile([P, NODES], F32, name="z_sb_%d_%d" % (b, t))
             nc.scalar.activation(out=z_sb[b, t][:], in_=z[b, t][:], func=ACT.Copy, accum_out=sums[:, b, t : t + 1])
 
+        def move_late(t):
+            z_sb[GRAPHS - 1, t] = keep.tile([P, NODES], F32, name="z_sb_late_%d" % t)
+            nc.scalar.copy(out=z_sb[GRAPHS - 1, t][:], in_=z[GRAPHS - 1, t][:])
+
         def means(b):
             nc.scalar.mul(out=scalar_triples[:, :, b, 1], in_=sums[:, b, :], mul=1.0 / NODES)
 
@@ -151,75 +155,58 @@ def tile_yuyipointupdate_pb_kernel(tc, h1, W2_words, W2_scales, g2, b2, out):
             first = SCALAR_GRAPHS * TRIPLE + (b - SCALAR_GRAPHS) * 2 * TRIPLE
             nc.vector.bn_stats(out=stats[:, t, first : first + 2 * TRIPLE], in_=z[b, t][:])
 
-        regroup_vector(0)
-        regroup_scalar(0)
+        def regroup(c):
+            regroup_vector(c)
+            regroup_scalar(c)
 
-        regroup_vector(1)
-        regroup_scalar(1)
+        regroup(0)
+        regroup(1)
         quantise(0)
         nc.scalar.copy(out=gb_square[0 : 2 * O_TILES, :], in_=gb_rows[:])
-
-        gb_bank = bank(5, [P, P], F32, "gb_bank")
+        gb_bank = bank(7, [P, P], F32, "gb_bank")
         nc.tensor.transpose(gb_bank[:], gb_square[:], identity[:])
-        regroup_vector(2)
-        regroup_scalar(2)
+        regroup(2)
         quantise(1)
-
         for t in range(O_TILES):
             multiply(0, t, t)
-        regroup_vector(3)
-        regroup_scalar(3)
+        regroup(3)
         quantise(2)
         nc.scalar.copy(out=gb[:], in_=gb_bank[:, 0 : 2 * O_TILES])
         move_out(0, 0)
         move_out(0, 1)
-
-        regroup_vector(4)
-        regroup_scalar(4)
+        regroup(4)
         quantise(3)
+        for t in range(O_TILES):
+            multiply(1, t, O_TILES + t)
         move_out(0, 2)
         move_out(0, 3)
-        means(0)
-
-        for t, k in enumerate((4, 5, 0, 1)):
-            multiply(1, t, k)
-        regroup_vector(5)
-        regroup_scalar(5)
+        regroup(5)
         quantise(4)
-        squares(0, 0)
-        squares(0, 1)
-
-        regroup_vector(6)
-        regroup_scalar(6)
+        regroup(6)
         quantise(5)
-
-        multiply(2, 0, 2)
-        multiply(2, 1, 3)
-        regroup_vector(7)
-        regroup_scalar(7)
+        for t in range(O_TILES):
+            multiply(2, t, t)
+        regroup(7)
         quantise(6)
         quantise(7)
-
-        move_out(1, 0)
-        move_out(1, 1)
-        multiply(2, 2, 4)
-        multiply(2, 3, 5)
-        move_out(1, 2)
-        move_out(1, 3)
-        for t, k in enumerate((6, 7, 0, 1)):
-            multiply(3, t, k)
+        for t in range(O_TILES):
+            move_out(1, t)
+        for t in range(O_TILES):
+            multiply(3, t, O_TILES + t)
+        means(0)
         means(1)
-        squares(0, 2)
-        squares(0, 3)
         for t in range(O_TILES):
             measure(2, t)
-            squares(1, t)
+            squares(0, t)
         for t in range(O_TILES):
+            squares(1, t)
             measure(3, t)
             nc.vector.bn_aggr(out=mean_var[:, t, :], in_=stats[:, t, :])
 
         rstd = keep.tile([P, O_TILES], F32, name="rstd")
+        move_late(0)
         nc.scalar.activation(out=rstd[:], in_=mean_var[:, :, 1], func=ACT.Abs_reciprocal_sqrt, bias=eps[:])
+        move_late(2)
         gain = keep.tile([P, O_TILES], F32, name="gain")
         nc.vector.tensor_mul(out=gain[:], in0=rstd[:], in1=gb[:, 0:O_TILES])
         mean_gain = keep.tile([P, O_TILES], F32, name="mean_gain")
@@ -227,31 +214,23 @@ def tile_yuyipointupdate_pb_kernel(tc, h1, W2_words, W2_scales, g2, b2, out):
         shift = keep.tile([P, O_TILES], F32, name="shift")
         nc.vector.tensor_sub(out=shift[:], in0=gb[:, O_TILES : 2 * O_TILES], in1=mean_gain[:])
 
-        def normalise(b):
-            for t in range(O_TILES):
-                y[b, t] = keep.tile([P, NODES], F32, name="y_%d_%d" % (b, t))
-                if b < SCALAR_GRAPHS:
-                    nc.gpsimd.tensor_scalar(
-                        out=y[b, t][:],
-                        in0=z_sb[b, t][:],
-                        scalar1=gain[:, t : t + 1],
-                        scalar2=shift[:, t : t + 1],
-                        op0=ALU.mult,
-                        op1=ALU.add,
-                    )
-                elif t % 2 == 0:
-                    nc.scalar.activation(
-                        out=y[b, t][:], in_=z[b, t][:], func=ACT.Identity, bias=shift[:, t : t + 1], scale=gain[:, t : t + 1]
-                    )
-                else:
-                    nc.vector.tensor_scalar(
-                        out=y[b, t][:],
-                        in0=z[b, t][:],
-                        scalar1=gain[:, t : t + 1],
-                        scalar2=shift[:, t : t + 1],
-                        op0=ALU.mult,
-                        op1=ALU.add,
-                    )
+        def normalise(b, t, engine):
+            y[b, t] = keep.tile([P, NODES], F32, name="y_%d_%d" % (b, t))
+            source = z_sb[b, t] if (b, t) in z_sb else z[b, t]
+            if engine == "scalar":
+                nc.scalar.activation(
+                    out=y[b, t][:], in_=source[:], func=ACT.Identity, bias=shift[:, t : t + 1], scale=gain[:, t : t + 1]
+                )
+            else:
+                builder = nc.vector if engine == "vector" else nc.gpsimd
+                builder.tensor_scalar(
+                    out=y[b, t][:],
+                    in0=source[:],
+                    scalar1=gain[:, t : t + 1],
+                    scalar2=shift[:, t : t + 1],
+                    op0=ALU.mult,
+                    op1=ALU.add,
+                )
 
         def finish(b, banks, last=False):
             turned = [bank(banks[j], [P, CHANNELS_OUT], F32, "turned_%d" % j) for j in range(N_TILES)]
@@ -271,11 +250,21 @@ def tile_yuyipointupdate_pb_kernel(tc, h1, W2_words, W2_scales, g2, b2, out):
                     )
                     nc.sync.dma_start(out=out[b, j * P : (j + 1) * P, o : o + width], in_=result[:, o : o + width])
 
-        normalise(2)
-        normalise(3)
-        normalise(0)
-        normalise(1)
-        finish(2, (2, 3, 4, 5))
-        finish(3, (6, 7, 0, 1))
-        finish(0, (2, 3, 4, 5))
-        finish(1, (6, 7, 0, 1), last=True)
+        normalise(2, 0, "scalar")
+        normalise(2, 1, "vector")
+        normalise(2, 2, "scalar")
+        normalise(2, 3, "vector")
+        normalise(3, 1, "scalar")
+        normalise(3, 3, "vector")
+        normalise(SCALAR_GRAPHS - 1, O_TILES - 2, "vector")
+        normalise(SCALAR_GRAPHS - 1, O_TILES - 1, "vector")
+        normalise(3, 0, "gpsimd")
+        normalise(3, 2, "gpsimd")
+        for b in range(SCALAR_GRAPHS):
+            for t in range(O_TILES):
+                if (b, t) not in y:
+                    normalise(b, t, "gpsimd")
+        finish(2, (0, 1, 2, 3))
+        finish(3, (4, 5, 6, 7))
+        finish(0, (0, 1, 2, 3))
+        finish(1, (4, 5, 6, 7), last=True)

@@ -214,18 +214,23 @@ def tile_yuyipointupdate_pb_kernel(tc, h1, W2_words, W2_scales, g2, b2, out):
         shift = keep.tile([P, O_TILES], F32, name="shift")
         nc.vector.tensor_sub(out=shift[:], in0=gb[:, O_TILES : 2 * O_TILES], in1=mean_gain[:])
 
-        def normalise(b, t, engine):
-            y[b, t] = keep.tile([P, NODES], F32, name="y_%d_%d" % (b, t))
+        def normalise(b, t, engine, nodes=slice(0, NODES)):
+            if (b, t) not in y:
+                y[b, t] = keep.tile([P, NODES], F32, name="y_%d_%d" % (b, t))
             source = z_sb[b, t] if (b, t) in z_sb else z[b, t]
             if engine == "scalar":
                 nc.scalar.activation(
-                    out=y[b, t][:], in_=source[:], func=ACT.Identity, bias=shift[:, t : t + 1], scale=gain[:, t : t + 1]
+                    out=y[b, t][:, nodes],
+                    in_=source[:, nodes],
+                    func=ACT.Identity,
+                    bias=shift[:, t : t + 1],
+                    scale=gain[:, t : t + 1],
                 )
             else:
                 builder = nc.vector if engine == "vector" else nc.gpsimd
                 builder.tensor_scalar(
-                    out=y[b, t][:],
-                    in0=source[:],
+                    out=y[b, t][:, nodes],
+                    in0=source[:, nodes],
                     scalar1=gain[:, t : t + 1],
                     scalar2=shift[:, t : t + 1],
                     op0=ALU.mult,
@@ -250,21 +255,19 @@ def tile_yuyipointupdate_pb_kernel(tc, h1, W2_words, W2_scales, g2, b2, out):
                     )
                     nc.sync.dma_start(out=out[b, j * P : (j + 1) * P, o : o + width], in_=result[:, o : o + width])
 
-        normalise(2, 0, "scalar")
-        normalise(2, 1, "vector")
-        normalise(2, 2, "scalar")
-        normalise(2, 3, "vector")
+        for nodes in (slice(0, P), slice(P, NODES)):
+            normalise(2, 0, "scalar", nodes)
+            normalise(2, 1, "vector", nodes)
+            normalise(2, 2, "scalar", nodes)
+            normalise(2, 3, "vector", nodes)
         normalise(3, 1, "scalar")
         normalise(3, 3, "vector")
-        normalise(SCALAR_GRAPHS - 1, O_TILES - 2, "vector")
-        normalise(SCALAR_GRAPHS - 1, O_TILES - 1, "vector")
         normalise(3, 0, "gpsimd")
         normalise(3, 2, "gpsimd")
         for b in range(SCALAR_GRAPHS):
             for t in range(O_TILES):
-                if (b, t) not in y:
-                    normalise(b, t, "gpsimd")
-        finish(2, (0, 1, 2, 3))
-        finish(3, (4, 5, 6, 7))
-        finish(0, (0, 1, 2, 3))
-        finish(1, (4, 5, 6, 7), last=True)
+                normalise(b, t, "gpsimd")
+        finish(2, (4, 6, 0, 1))
+        finish(3, (2, 3, 5, 7))
+        finish(0, (4, 6, 0, 1))
+        finish(1, (2, 3, 5, 7), last=True)

@@ -237,23 +237,17 @@ def tile_yuyipointupdate_pb_kernel(tc, h1, W2_words, W2_scales, g2, b2, out):
                     op1=ALU.add,
                 )
 
-        def finish(b, banks, last=False):
+        def finish(b, banks):
             turned = [bank(banks[j], [P, CHANNELS_OUT], F32, "turned_%d" % j) for j in range(N_TILES)]
             for j in range(N_TILES):
                 for t in range(O_TILES):
                     nc.tensor.transpose(turned[j][:, t * P : (t + 1) * P], y[b, t][:, j * P : (j + 1) * P], identity[:])
             for j in range(N_TILES):
                 sloped = work.tile([P, CHANNELS_OUT], F32, name="sloped")
+                nc.scalar.mul(out=sloped[:], in_=turned[j][:], mul=NEG_SLOPE)
                 result = work.tile([P, CHANNELS_OUT], F32, name="result")
-                pieces = 2 if last and j == N_TILES - 1 else 1
-                width = CHANNELS_OUT // pieces
-                for o in range(0, CHANNELS_OUT, width):
-                    nc.scalar.mul(out=sloped[:, o : o + width], in_=turned[j][:, o : o + width], mul=NEG_SLOPE)
-                for o in range(0, CHANNELS_OUT, width):
-                    nc.vector.tensor_tensor(
-                        out=result[:, o : o + width], in0=turned[j][:, o : o + width], in1=sloped[:, o : o + width], op=ALU.max
-                    )
-                    nc.sync.dma_start(out=out[b, j * P : (j + 1) * P, o : o + width], in_=result[:, o : o + width])
+                nc.vector.tensor_tensor(out=result[:], in0=turned[j][:], in1=sloped[:], op=ALU.max)
+                nc.sync.dma_start(out=out[b, j * P : (j + 1) * P, :], in_=result[:])
 
         for nodes in (slice(0, P), slice(P, NODES)):
             normalise(2, 0, "scalar", nodes)
@@ -270,4 +264,4 @@ def tile_yuyipointupdate_pb_kernel(tc, h1, W2_words, W2_scales, g2, b2, out):
         finish(2, (4, 6, 0, 1))
         finish(3, (2, 3, 5, 7))
         finish(0, (4, 6, 0, 1))
-        finish(1, (2, 3, 5, 7), last=True)
+        finish(1, (2, 3, 5, 7))

@@ -28,7 +28,7 @@ NEG_SLOPE = 0.01
 FLOPS = 2 * GRAPHS * NODES * CHANNELS_IN * CHANNELS_OUT
 
 RUN = 4
-VECTOR_RUNS_EARLY = 76
+VECTOR_RUNS_EARLY = 68
 VECTOR_RUNS_LATE = 100
 EARLY_CHUNKS = 4
 SCALAR_GRAPHS = 2
@@ -48,25 +48,24 @@ def tile_yuyipointupdate_pb_kernel(tc, h1, W2_words, W2_scales, g2, b2, out):
         def bank(k, shape, dtype, name):
             return psum.tile(shape, dtype, tag="bank%d" % k, name=name)
 
+        raw = {}
         w_planes = keep.tile([P, PASSES, CHANNELS_OUT], U8, name="w_planes", align_bytes=64)
         nc.vector.memset(w_planes[:].bitcast(I32), 0)
         gb_rows = keep.tile([2 * O_TILES, P], BF16, name="gb_rows")
-        nc.scalar.dma_start(out=gb_rows[0:O_TILES, :], in_=g2.rearrange("(t m) -> t m", m=P))
-        nc.scalar.dma_start(out=gb_rows[O_TILES : 2 * O_TILES, :], in_=b2.rearrange("(t m) -> t m", m=P))
-        for quadrant in range(4):
-            nc.scalar.dma_start(
-                out=w_planes[32 * quadrant : 32 * quadrant + 4, :, :].bitcast(F32),
-                in_=W2_scales.bitcast(F32)[:, 4 * quadrant : 4 * quadrant + 4, :].rearrange("g r m -> r g m"),
-            )
-
-        raw = {}
-
         w_words = keep.tile([P, PASSES, 2 * CHANNELS_OUT], U8, name="w_words", align_bytes=64)
         for c in range(GRAPHS * PASSES):
             b, g = c // PASSES, c % PASSES
             raw[c] = keep.tile([P, PACK, NODES], BF16, name="raw_%d" % c)
             rows = h1[b, g * K_PASS : (g + 1) * K_PASS, :]
             nc.sync.dma_start(out=raw[c][:], in_=rows.rearrange("(p t) n -> p t n", t=PACK))
+            if c == 1:
+                nc.sync.dma_start(out=gb_rows[0:O_TILES, :], in_=g2.rearrange("(t m) -> t m", m=P))
+                nc.sync.dma_start(out=gb_rows[O_TILES : 2 * O_TILES, :], in_=b2.rearrange("(t m) -> t m", m=P))
+                for quadrant in range(4):
+                    nc.sync.dma_start(
+                        out=w_planes[32 * quadrant : 32 * quadrant + 4, :, :].bitcast(I32),
+                        in_=W2_scales.bitcast(I32)[:, 4 * quadrant : 4 * quadrant + 4, :].rearrange("g r m -> r g m"),
+                    )
             if c == PASSES:
                 nc.sync.dma_start(out=w_words[:].bitcast(I32), in_=W2_words.bitcast(I32).rearrange("g p m -> p g m"))
 
@@ -133,10 +132,6 @@ def tile_yuyipointupdate_pb_kernel(tc, h1, W2_words, W2_scales, g2, b2, out):
             z_sb[b, t] = keep.tile([P, NODES], F32, name="z_sb_%d_%d" % (b, t))
             nc.scalar.activation(out=z_sb[b, t][:], in_=z[b, t][:], func=ACT.Copy, accum_out=sums[:, b, t : t + 1])
 
-        def move_late(t):
-            z_sb[GRAPHS - 1, t] = keep.tile([P, NODES], F32, name="z_sb_late_%d" % t)
-            nc.scalar.copy(out=z_sb[GRAPHS - 1, t][:], in_=z[GRAPHS - 1, t][:])
-
         def means(b):
             nc.scalar.mul(out=scalar_triples[:, :, b, 1], in_=sums[:, b, :], mul=1.0 / NODES)
 
@@ -195,73 +190,108 @@ def tile_yuyipointupdate_pb_kernel(tc, h1, W2_words, W2_scales, g2, b2, out):
             multiply(3, t, O_TILES + t)
         means(0)
         means(1)
-        for t in range(O_TILES):
-            measure(2, t)
-            squares(0, t)
-        for t in range(O_TILES):
-            squares(1, t)
-            measure(3, t)
-            nc.vector.bn_aggr(out=mean_var[:, t, :], in_=stats[:, t, :])
 
         rstd = keep.tile([P, O_TILES], F32, name="rstd")
-        move_late(0)
-        nc.scalar.activation(out=rstd[:], in_=mean_var[:, :, 1], func=ACT.Abs_reciprocal_sqrt, bias=eps[:])
-        move_late(2)
         gain = keep.tile([P, O_TILES], F32, name="gain")
-        nc.vector.tensor_mul(out=gain[:], in0=rstd[:], in1=gb[:, 0:O_TILES])
         mean_gain = keep.tile([P, O_TILES], F32, name="mean_gain")
-        nc.vector.tensor_mul(out=mean_gain[:], in0=mean_var[:, :, 0], in1=gain[:])
         shift = keep.tile([P, O_TILES], F32, name="shift")
-        nc.vector.tensor_sub(out=shift[:], in0=gb[:, O_TILES : 2 * O_TILES], in1=mean_gain[:])
 
-        def normalise(b, t, engine, nodes=slice(0, NODES)):
-            if (b, t) not in y:
-                y[b, t] = keep.tile([P, NODES], F32, name="y_%d_%d" % (b, t))
+        def aggregate(t):
+            nc.vector.bn_aggr(out=mean_var[:, t, :], in_=stats[:, t, :])
+
+        def reciprocal_roots(tiles):
+            nc.scalar.activation(out=rstd[:, tiles], in_=mean_var[:, tiles, 1], func=ACT.Abs_reciprocal_sqrt, bias=eps[:])
+
+        def gains(tiles):
+            nc.vector.tensor_mul(out=gain[:, tiles], in0=rstd[:, tiles], in1=gb[:, tiles])
+            nc.vector.tensor_mul(out=mean_gain[:, tiles], in0=mean_var[:, tiles, 0], in1=gain[:, tiles])
+            nc.vector.tensor_sub(
+                out=shift[:, tiles],
+                in0=gb[:, O_TILES + tiles.start : O_TILES + tiles.stop],
+                in1=mean_gain[:, tiles],
+            )
+
+        def normalise(b, t, engine):
+            y[b, t] = keep.tile([P, NODES], F32, name="y_%d_%d" % (b, t))
             source = z_sb[b, t] if (b, t) in z_sb else z[b, t]
             if engine == "scalar":
                 nc.scalar.activation(
-                    out=y[b, t][:, nodes],
-                    in_=source[:, nodes],
-                    func=ACT.Identity,
-                    bias=shift[:, t : t + 1],
-                    scale=gain[:, t : t + 1],
+                    out=y[b, t][:], in_=source[:], func=ACT.Identity, bias=shift[:, t : t + 1], scale=gain[:, t : t + 1]
                 )
             else:
                 builder = nc.vector if engine == "vector" else nc.gpsimd
                 builder.tensor_scalar(
-                    out=y[b, t][:, nodes],
-                    in0=source[:, nodes],
+                    out=y[b, t][:],
+                    in0=source[:],
                     scalar1=gain[:, t : t + 1],
                     scalar2=shift[:, t : t + 1],
                     op0=ALU.mult,
                     op1=ALU.add,
                 )
 
-        def finish(b, banks):
-            turned = [bank(banks[j], [P, CHANNELS_OUT], F32, "turned_%d" % j) for j in range(N_TILES)]
+        def turn(b, banks):
             for j in range(N_TILES):
+                turned[b, j] = bank(banks[j], [P, CHANNELS_OUT], F32, "turned")
                 for t in range(O_TILES):
-                    nc.tensor.transpose(turned[j][:, t * P : (t + 1) * P], y[b, t][:, j * P : (j + 1) * P], identity[:])
-            for j in range(N_TILES):
-                sloped = work.tile([P, CHANNELS_OUT], F32, name="sloped")
-                nc.scalar.mul(out=sloped[:], in_=turned[j][:], mul=NEG_SLOPE)
-                result = work.tile([P, CHANNELS_OUT], F32, name="result")
-                nc.vector.tensor_tensor(out=result[:], in0=turned[j][:], in1=sloped[:], op=ALU.max)
-                nc.sync.dma_start(out=out[b, j * P : (j + 1) * P, :], in_=result[:])
+                    nc.tensor.transpose(turned[b, j][:, t * P : (t + 1) * P], y[b, t][:, j * P : (j + 1) * P], identity[:])
 
-        for nodes in (slice(0, P), slice(P, NODES)):
-            normalise(2, 0, "scalar", nodes)
-            normalise(2, 1, "vector", nodes)
-            normalise(2, 2, "scalar", nodes)
-            normalise(2, 3, "vector", nodes)
-        normalise(3, 1, "scalar")
-        normalise(3, 3, "vector")
-        normalise(3, 0, "gpsimd")
-        normalise(3, 2, "gpsimd")
+        def leave(b, j):
+            sloped = work.tile([P, CHANNELS_OUT], F32, name="sloped")
+            nc.scalar.mul(out=sloped[:], in_=turned[b, j][:], mul=NEG_SLOPE)
+            result = work.tile([P, CHANNELS_OUT], F32, name="result")
+            nc.vector.tensor_tensor(out=result[:], in0=turned[b, j][:], in1=sloped[:], op=ALU.max)
+            nc.sync.dma_start(out=out[b, j * P : (j + 1) * P, :], in_=result[:])
+
+        turned = {}
+        first, second = slice(0, 2), slice(2, 4)
+        for t in (0, 1):
+            measure(2, t)
+            squares(0, t)
+            squares(1, t)
+        for t in (0, 1):
+            measure(3, t)
+        aggregate(0)
+        aggregate(1)
+        measure(2, 2)
+        squares(0, 2)
+        reciprocal_roots(first)
+        squares(1, 2)
+        gains(first)
         for b in range(SCALAR_GRAPHS):
-            for t in range(O_TILES):
-                normalise(b, t, "gpsimd")
-        finish(2, (4, 6, 0, 1))
-        finish(3, (2, 3, 5, 7))
-        finish(0, (4, 6, 0, 1))
-        finish(1, (2, 3, 5, 7))
+            normalise(b, 0, "gpsimd")
+            normalise(b, 1, "gpsimd")
+        measure(2, 3)
+        squares(0, 3)
+        squares(1, 3)
+        measure(3, 2)
+        measure(3, 3)
+        aggregate(2)
+        aggregate(3)
+        normalise(2, 0, "vector")
+        normalise(2, 1, "scalar")
+        reciprocal_roots(second)
+        gains(second)
+        normalise(3, 0, "scalar")
+        normalise(3, 1, "scalar")
+        normalise(0, 2, "vector")
+        normalise(0, 3, "vector")
+        normalise(1, 2, "gpsimd")
+        normalise(1, 3, "gpsimd")
+        turn(0, (0, 1, 4, 5))
+        normalise(2, 2, "scalar")
+        normalise(2, 3, "vector")
+        normalise(3, 3, "vector")
+        leave(0, 0)
+        normalise(3, 2, "scalar")
+        leave(0, 1)
+        leave(0, 2)
+        turn(2, (2, 3, 6, 7))
+        leave(0, 3)
+        for j in range(N_TILES):
+            leave(2, j)
+        turn(1, (0, 1, 4, 5))
+        for j in range(N_TILES):
+            leave(1, j)
+        turn(3, (2, 3, 6, 7))
+        for j in range(N_TILES):
+            leave(3, j)

@@ -28,12 +28,12 @@ NEG_SLOPE = 0.01
 FLOPS = 2 * GRAPHS * NODES * CHANNELS_IN * CHANNELS_OUT
 
 RUN = 4
-VECTOR_RUNS_EARLY = 68
-VECTOR_RUNS_LATE = 100
+VECTOR_RUNS_EARLY = 64
+VECTOR_RUNS_LATE = 96
 EARLY_CHUNKS = 4
 SCALAR_GRAPHS = 2
 TRIPLE = 3
-STATS_WIDTH = SCALAR_GRAPHS * TRIPLE + (GRAPHS - SCALAR_GRAPHS) * 2 * TRIPLE
+STATS_WIDTH = TRIPLE + (GRAPHS - SCALAR_GRAPHS) * 2 * TRIPLE
 
 
 def tile_yuyipointupdate_pb_kernel(tc, h1, W2_words, W2_scales, g2, b2, out):
@@ -48,6 +48,8 @@ def tile_yuyipointupdate_pb_kernel(tc, h1, W2_words, W2_scales, g2, b2, out):
         def bank(k, shape, dtype, name):
             return psum.tile(shape, dtype, tag="bank%d" % k, name=name)
 
+        identity = keep.tile([P, P], F32, name="identity")
+        masks.make_identity(nc, identity[:])
         raw = {}
         w_planes = keep.tile([P, PASSES, CHANNELS_OUT], U8, name="w_planes", align_bytes=64)
         nc.vector.memset(w_planes[:].bitcast(I32), 0)
@@ -61,28 +63,28 @@ def tile_yuyipointupdate_pb_kernel(tc, h1, W2_words, W2_scales, g2, b2, out):
             if c == 1:
                 nc.sync.dma_start(out=gb_rows[0:O_TILES, :], in_=g2.rearrange("(t m) -> t m", m=P))
                 nc.sync.dma_start(out=gb_rows[O_TILES : 2 * O_TILES, :], in_=b2.rearrange("(t m) -> t m", m=P))
+            if c == 3:
                 for quadrant in range(4):
                     nc.sync.dma_start(
                         out=w_planes[32 * quadrant : 32 * quadrant + 4, :, :].bitcast(I32),
                         in_=W2_scales.bitcast(I32)[:, 4 * quadrant : 4 * quadrant + 4, :].rearrange("g r m -> r g m"),
                     )
-            if c == PASSES:
                 nc.sync.dma_start(out=w_words[:].bitcast(I32), in_=W2_words.bitcast(I32).rearrange("g p m -> p g m"))
 
         eps = keep.tile([P, 1], F32, name="eps")
         nc.vector.memset(eps[:], EPS_BN)
         warm = keep.tile([P, 1], F32, name="warm")
         nc.scalar.activation(out=warm[:], in_=eps[:], func=ACT.Abs_reciprocal_sqrt)
-        identity = keep.tile([P, P], F32, name="identity")
-        masks.make_identity(nc, identity[:])
         gb_square = keep.tile([P, P], F32, name="gb_square")
         nc.vector.memset(gb_square[:], 0.0)
         gb = keep.tile([P, 2 * O_TILES], F32, name="gb")
 
         stats = keep.tile([P, O_TILES, STATS_WIDTH], F32, name="stats")
-        scalar_triples = stats[:, :, 0 : SCALAR_GRAPHS * TRIPLE].rearrange("p t (b s) -> p t b s", s=TRIPLE)
-        nc.vector.memset(scalar_triples[:, :, :, 0:1], float(NODES))
+        nc.vector.memset(stats[:, :, 0:1], float(SCALAR_GRAPHS * NODES))
         sums = keep.tile([P, SCALAR_GRAPHS, O_TILES], F32, name="sums")
+        both = keep.tile([P, O_TILES], F32, name="both")
+        mean = keep.tile([P, O_TILES], F32, name="mean")
+        z_kept = [keep.tile([P, SCALAR_GRAPHS, NODES], F32, name="z_kept_%d" % t) for t in range(O_TILES)]
         mean_var = keep.tile([P, O_TILES, 2], F32, name="mean_var")
 
         grouped = {}
@@ -129,26 +131,39 @@ def tile_yuyipointupdate_pb_kernel(tc, h1, W2_words, W2_scales, g2, b2, out):
                 )
 
         def move_out(b, t):
-            z_sb[b, t] = keep.tile([P, NODES], F32, name="z_sb_%d_%d" % (b, t))
-            nc.scalar.activation(out=z_sb[b, t][:], in_=z[b, t][:], func=ACT.Copy, accum_out=sums[:, b, t : t + 1])
+            z_sb[b, t] = z_kept[t][:, b, :]
+            nc.scalar.activation(out=z_sb[b, t], in_=z[b, t][:], func=ACT.Copy, accum_out=sums[:, b, t : t + 1])
 
-        def means(b):
-            nc.scalar.mul(out=scalar_triples[:, :, b, 1], in_=sums[:, b, :], mul=1.0 / NODES)
+        def means(tiles):
+            nc.gpsimd.tensor_tensor(out=both[:, tiles], in0=sums[:, 0, tiles], in1=sums[:, 1, tiles], op=ALU.add)
+            nc.gpsimd.tensor_scalar(
+                out=mean[:, tiles],
+                in0=both[:, tiles],
+                scalar1=1.0 / (SCALAR_GRAPHS * NODES),
+                scalar2=0.0,
+                op0=ALU.mult,
+                op1=ALU.add,
+            )
 
-        def squares(b, t):
-            junk = work.tile([P, NODES], F32, name="junk")
+        def keep_means(tiles):
+            nc.scalar.copy(out=stats[:, tiles, 1], in_=mean[:, tiles])
+
+        def squares(t):
+            junk = work.tile([P, SCALAR_GRAPHS, NODES], F32, name="junk")
             nc.scalar.activation(
                 out=junk[:],
-                in_=z_sb[b, t][:],
+                in_=z_kept[t][:],
                 func=ACT.Square,
                 scale=-1.0,
-                bias=scalar_triples[:, t, b, 1:2],
-                accum_out=scalar_triples[:, t, b, 2:3],
+                bias=mean[:, t : t + 1],
+                accum_out=stats[:, t, 2:3],
             )
 
         def measure(b, t):
-            first = SCALAR_GRAPHS * TRIPLE + (b - SCALAR_GRAPHS) * 2 * TRIPLE
-            nc.vector.bn_stats(out=stats[:, t, first : first + 2 * TRIPLE], in_=z[b, t][:])
+            start = TRIPLE + (b - SCALAR_GRAPHS) * 2 * TRIPLE
+            nc.vector.bn_stats(out=stats[:, t, start : start + 2 * TRIPLE], in_=z[b, t][:])
+
+        first, second = slice(0, 2), slice(2, 4)
 
         def regroup(c):
             regroup_vector(c)
@@ -184,12 +199,12 @@ def tile_yuyipointupdate_pb_kernel(tc, h1, W2_words, W2_scales, g2, b2, out):
         regroup(7)
         quantise(6)
         quantise(7)
-        for t in range(O_TILES):
-            move_out(1, t)
+        for tiles in (first, second):
+            for t in range(tiles.start, tiles.stop):
+                move_out(1, t)
+            means(tiles)
         for t in range(O_TILES):
             multiply(3, t, O_TILES + t)
-        means(0)
-        means(1)
 
         rstd = keep.tile([P, O_TILES], F32, name="rstd")
         gain = keep.tile([P, O_TILES], F32, name="gain")
@@ -211,18 +226,21 @@ def tile_yuyipointupdate_pb_kernel(tc, h1, W2_words, W2_scales, g2, b2, out):
                 in1=mean_gain[:, tiles],
             )
 
+        turned = {}
+
         def normalise(b, t, engine):
-            y[b, t] = keep.tile([P, NODES], F32, name="y_%d_%d" % (b, t))
-            source = z_sb[b, t] if (b, t) in z_sb else z[b, t]
+            slot = 0 if b == 1 and t >= 2 else b
+            y[b, t] = keep.tile([P, NODES], F32, name="y_%d_%d" % (slot, t), tag="y_%d_%d" % (slot, t))
+            source = z_sb[b, t] if (b, t) in z_sb else z[b, t][:]
             if engine == "scalar":
                 nc.scalar.activation(
-                    out=y[b, t][:], in_=source[:], func=ACT.Identity, bias=shift[:, t : t + 1], scale=gain[:, t : t + 1]
+                    out=y[b, t][:], in_=source, func=ACT.Identity, bias=shift[:, t : t + 1], scale=gain[:, t : t + 1]
                 )
             else:
                 builder = nc.vector if engine == "vector" else nc.gpsimd
                 builder.tensor_scalar(
                     out=y[b, t][:],
-                    in0=source[:],
+                    in0=source,
                     scalar1=gain[:, t : t + 1],
                     scalar2=shift[:, t : t + 1],
                     op0=ALU.mult,
@@ -242,28 +260,25 @@ def tile_yuyipointupdate_pb_kernel(tc, h1, W2_words, W2_scales, g2, b2, out):
             nc.vector.tensor_tensor(out=result[:], in0=turned[b, j][:], in1=sloped[:], op=ALU.max)
             nc.sync.dma_start(out=out[b, j * P : (j + 1) * P, :], in_=result[:])
 
-        turned = {}
-        first, second = slice(0, 2), slice(2, 4)
-        for t in (0, 1):
-            measure(2, t)
-            squares(0, t)
-            squares(1, t)
-        for t in (0, 1):
-            measure(3, t)
+        measure(2, 0)
+        squares(0)
+        measure(2, 1)
+        squares(1)
+        keep_means(first)
+        measure(3, 0)
+        measure(3, 1)
+        measure(2, 2)
+        squares(2)
+        measure(2, 3)
         aggregate(0)
         aggregate(1)
-        measure(2, 2)
-        squares(0, 2)
         reciprocal_roots(first)
-        squares(1, 2)
-        gains(first)
-        for b in range(SCALAR_GRAPHS):
-            normalise(b, 0, "gpsimd")
-            normalise(b, 1, "gpsimd")
-        measure(2, 3)
-        squares(0, 3)
-        squares(1, 3)
+        keep_means(second)
+        squares(3)
         measure(3, 2)
+        gains(first)
+        normalise(0, 0, "gpsimd")
+        normalise(0, 1, "gpsimd")
         measure(3, 3)
         aggregate(2)
         aggregate(3)
@@ -275,9 +290,11 @@ def tile_yuyipointupdate_pb_kernel(tc, h1, W2_words, W2_scales, g2, b2, out):
         normalise(3, 1, "scalar")
         normalise(0, 2, "vector")
         normalise(0, 3, "vector")
+        turn(0, (0, 1, 4, 5))
         normalise(1, 2, "gpsimd")
         normalise(1, 3, "gpsimd")
-        turn(0, (0, 1, 4, 5))
+        normalise(1, 0, "gpsimd")
+        normalise(1, 1, "gpsimd")
         normalise(2, 2, "scalar")
         normalise(2, 3, "vector")
         normalise(3, 3, "vector")
@@ -287,11 +304,17 @@ def tile_yuyipointupdate_pb_kernel(tc, h1, W2_words, W2_scales, g2, b2, out):
         leave(0, 2)
         turn(2, (2, 3, 6, 7))
         leave(0, 3)
-        for j in range(N_TILES):
-            leave(2, j)
-        turn(1, (0, 1, 4, 5))
-        for j in range(N_TILES):
-            leave(1, j)
-        turn(3, (2, 3, 6, 7))
-        for j in range(N_TILES):
-            leave(3, j)
+        leave(2, 0)
+        leave(2, 1)
+        leave(2, 2)
+        leave(2, 3)
+        turn(3, (0, 1, 4, 5))
+        leave(3, 0)
+        leave(3, 1)
+        leave(3, 2)
+        leave(3, 3)
+        turn(1, (2, 3, 6, 7))
+        leave(1, 0)
+        leave(1, 1)
+        leave(1, 2)
+        leave(1, 3)

@@ -31,6 +31,7 @@ RUN = 4
 VECTOR_RUNS_EARLY = 64
 VECTOR_RUNS_LATE = 96
 EARLY_CHUNKS = 4
+WARM_UP = 14
 SCALAR_GRAPHS = 2
 TRIPLE = 3
 STATS_WIDTH = TRIPLE + (GRAPHS - SCALAR_GRAPHS) * 2 * TRIPLE
@@ -86,6 +87,10 @@ def tile_yuyipointupdate_pb_kernel(tc, h1, W2_words, W2_scales, g2, b2, out):
         mean = keep.tile([P, O_TILES], F32, name="mean")
         z_kept = [keep.tile([P, SCALAR_GRAPHS, NODES], F32, name="z_kept_%d" % t) for t in range(O_TILES)]
         mean_var = keep.tile([P, O_TILES, 2], F32, name="mean_var")
+
+        idle_bank = bank(6, [P, P], F32, "idle_bank")
+        for i in range(WARM_UP):
+            nc.tensor.matmul(out=idle_bank[:], lhsT=identity[:], rhs=identity[:], start=True, stop=True)
 
         grouped = {}
         codes = {}

@@ -234,17 +234,17 @@ def tile_yuyipointupdate_pb_kernel(tc, h1, W2_words, W2_scales, g2, b2, out):
         turned = {}
 
         def normalise(b, t, engine):
-            slot = 0 if b == 1 and t >= 2 else b
-            y[b, t] = keep.tile([P, NODES], F32, name="y_%d_%d" % (slot, t), tag="y_%d_%d" % (slot, t))
+            if b not in y:
+                y[b] = keep.tile([P, O_TILES, NODES], F32, name="y_%d" % b, tag="y_%d" % (0 if b == 1 else b))
             source = z_sb[b, t] if (b, t) in z_sb else z[b, t][:]
             if engine == "scalar":
                 nc.scalar.activation(
-                    out=y[b, t][:], in_=source, func=ACT.Identity, bias=shift[:, t : t + 1], scale=gain[:, t : t + 1]
+                    out=y[b][:, t, :], in_=source, func=ACT.Identity, bias=shift[:, t : t + 1], scale=gain[:, t : t + 1]
                 )
             else:
                 builder = nc.vector if engine == "vector" else nc.gpsimd
                 builder.tensor_scalar(
-                    out=y[b, t][:],
+                    out=y[b][:, t, :],
                     in0=source,
                     scalar1=gain[:, t : t + 1],
                     scalar2=shift[:, t : t + 1],
@@ -256,7 +256,7 @@ def tile_yuyipointupdate_pb_kernel(tc, h1, W2_words, W2_scales, g2, b2, out):
             for j in range(N_TILES):
                 turned[b, j] = bank(banks[j], [P, CHANNELS_OUT], F32, "turned")
                 for t in range(O_TILES):
-                    nc.tensor.transpose(turned[b, j][:, t * P : (t + 1) * P], y[b, t][:, j * P : (j + 1) * P], identity[:])
+                    nc.tensor.transpose(turned[b, j][:, t * P : (t + 1) * P], y[b][:, t, j * P : (j + 1) * P], identity[:])
 
         def leave(b, j):
             sloped = work.tile([P, CHANNELS_OUT], F32, name="sloped")
@@ -264,6 +264,27 @@ def tile_yuyipointupdate_pb_kernel(tc, h1, W2_words, W2_scales, g2, b2, out):
             result = work.tile([P, CHANNELS_OUT], F32, name="result")
             nc.vector.tensor_tensor(out=result[:], in0=turned[b, j][:], in1=sloped[:], op=ALU.max)
             nc.sync.dma_start(out=out[b, j * P : (j + 1) * P, :], in_=result[:])
+
+        def turn_half(b, half, banks):
+            for i in range(2):
+                turned[b, half, i] = bank(banks[i], [P, 2, 2 * P], F32, "turned_half")
+                for j in range(2):
+                    for t in range(2):
+                        nc.tensor.transpose(
+                            turned[b, half, i][:, j, t * P : (t + 1) * P],
+                            y[b][:, 2 * half + t, (2 * i + j) * P : (2 * i + j + 1) * P],
+                            identity[:],
+                        )
+
+        def leave_half(b, half, i):
+            sloped = work.tile([P, 2, 2 * P], F32, name="sloped_half")
+            nc.scalar.mul(out=sloped[:], in_=turned[b, half, i][:], mul=NEG_SLOPE)
+            result = work.tile([P, 2, 2 * P], F32, name="result_half")
+            nc.vector.tensor_tensor(out=result[:], in0=turned[b, half, i][:], in1=sloped[:], op=ALU.max)
+            nc.sync.dma_start(
+                out=out[b, 2 * i * P : 2 * (i + 1) * P, 2 * half * P : 2 * (half + 1) * P].rearrange("(j p) c -> p j c", p=P),
+                in_=result[:],
+            )
 
         measure(2, 0)
         squares(0)
@@ -274,41 +295,42 @@ def tile_yuyipointupdate_pb_kernel(tc, h1, W2_words, W2_scales, g2, b2, out):
         measure(3, 1)
         measure(2, 2)
         squares(2)
-        measure(2, 3)
         aggregate(0)
         aggregate(1)
         reciprocal_roots(first)
         keep_means(second)
-        squares(3)
-        measure(3, 2)
+        measure(2, 3)
         gains(first)
         normalise(0, 0, "gpsimd")
         normalise(0, 1, "gpsimd")
+        squares(3)
+        measure(3, 2)
         measure(3, 3)
         aggregate(2)
         aggregate(3)
-        normalise(2, 0, "vector")
-        normalise(2, 1, "scalar")
+        normalise(2, 0, "scalar")
+        normalise(2, 1, "vector")
         reciprocal_roots(second)
+        turn_half(0, 0, (0, 1))
         gains(second)
         normalise(3, 0, "scalar")
-        normalise(3, 1, "scalar")
         normalise(0, 2, "vector")
         normalise(0, 3, "vector")
-        turn(0, (0, 1, 4, 5))
+        leave_half(0, 0, 0)
+        normalise(3, 1, "scalar")
+        normalise(2, 2, "vector")
+        leave_half(0, 0, 1)
+        turn_half(0, 1, (4, 5))
         normalise(1, 2, "gpsimd")
         normalise(1, 3, "gpsimd")
         normalise(1, 0, "gpsimd")
         normalise(1, 1, "gpsimd")
-        normalise(2, 2, "scalar")
-        normalise(2, 3, "vector")
+        normalise(2, 3, "scalar")
         normalise(3, 3, "vector")
-        leave(0, 0)
+        leave_half(0, 1, 0)
         normalise(3, 2, "scalar")
-        leave(0, 1)
-        leave(0, 2)
+        leave_half(0, 1, 1)
         turn(2, (2, 3, 6, 7))
-        leave(0, 3)
         leave(2, 0)
         leave(2, 1)
         leave(2, 2)

@@ -29,9 +29,10 @@ FLOPS = 2 * GRAPHS * NODES * CHANNELS_IN * CHANNELS_OUT
 
 RUN = 4
 VECTOR_RUNS_EARLY = 64
-VECTOR_RUNS_LATE = 96
+VECTOR_RUNS_LATE = 100
 EARLY_CHUNKS = 4
 WARM_UP = 14
+KEEP_BUSY = 3
 SCALAR_GRAPHS = 2
 TRIPLE = 3
 STATS_WIDTH = TRIPLE + (GRAPHS - SCALAR_GRAPHS) * 2 * TRIPLE
@@ -122,9 +123,9 @@ def tile_yuyipointupdate_pb_kernel(tc, h1, W2_words, W2_scales, g2, b2, out):
                 in_=grouped[c][:].rearrange("p n t -> p (n t)"),
             )
 
-        def multiply(b, t, k):
+        def multiply(b, t, k, times=1):
             z[b, t] = bank(k, [P, NODES], F32, "z")
-            for g in range(PASSES):
+            for g in list(range(PASSES)) * times:
                 nc.tensor.matmul_mx(
                     out=z[b, t][:],
                     lhsT=w_words[:, g, 2 * P * t : 2 * P * (t + 1)].bitcast(FP4X4),
@@ -209,10 +210,11 @@ def tile_yuyipointupdate_pb_kernel(tc, h1, W2_words, W2_scales, g2, b2, out):
                 move_out(1, t)
             means(tiles)
         for t in range(O_TILES):
-            multiply(3, t, O_TILES + t)
+            multiply(3, t, O_TILES + t, KEEP_BUSY if t == O_TILES - 1 else 1)
 
         rstd = keep.tile([P, O_TILES], F32, name="rstd")
         gain = keep.tile([P, O_TILES], F32, name="gain")
+        mean_g2 = {h: keep.tile([P, O_TILES // 2], F32, name="mean_g2_%d" % h) for h in (0, 2)}
         mean_gain = keep.tile([P, O_TILES], F32, name="mean_gain")
         shift = keep.tile([P, O_TILES], F32, name="shift")
 
@@ -222,10 +224,13 @@ def tile_yuyipointupdate_pb_kernel(tc, h1, W2_words, W2_scales, g2, b2, out):
         def reciprocal_roots(tiles):
             nc.scalar.activation(out=rstd[:, tiles], in_=mean_var[:, tiles, 1], func=ACT.Abs_reciprocal_sqrt, bias=eps[:])
 
-        def gains(tiles):
-            nc.vector.tensor_mul(out=gain[:, tiles], in0=rstd[:, tiles], in1=gb[:, tiles])
-            nc.vector.tensor_mul(out=mean_gain[:, tiles], in0=mean_var[:, tiles, 0], in1=gain[:, tiles])
-            nc.vector.tensor_sub(
+        def mean_times_g2(tiles, builder):
+            builder.tensor_mul(out=mean_g2[tiles.start][:], in0=mean_var[:, tiles, 0], in1=gb[:, tiles])
+
+        def gains(tiles, builder):
+            builder.tensor_mul(out=mean_gain[:, tiles], in0=mean_g2[tiles.start][:], in1=rstd[:, tiles])
+            builder.tensor_mul(out=gain[:, tiles], in0=gb[:, tiles], in1=rstd[:, tiles])
+            builder.tensor_sub(
                 out=shift[:, tiles],
                 in0=gb[:, O_TILES + tiles.start : O_TILES + tiles.stop],
                 in1=mean_gain[:, tiles],
@@ -268,8 +273,8 @@ def tile_yuyipointupdate_pb_kernel(tc, h1, W2_words, W2_scales, g2, b2, out):
         def turn_half(b, half, banks):
             for i in range(2):
                 turned[b, half, i] = bank(banks[i], [P, 2, 2 * P], F32, "turned_half")
-                for j in range(2):
-                    for t in range(2):
+                for t in range(2):
+                    for j in range(2):
                         nc.tensor.transpose(
                             turned[b, half, i][:, j, t * P : (t + 1) * P],
                             y[b][:, 2 * half + t, (2 * i + j) * P : (2 * i + j + 1) * P],
@@ -297,10 +302,11 @@ def tile_yuyipointupdate_pb_kernel(tc, h1, W2_words, W2_scales, g2, b2, out):
         squares(2)
         aggregate(0)
         aggregate(1)
+        mean_times_g2(first, nc.gpsimd)
         reciprocal_roots(first)
         keep_means(second)
         measure(2, 3)
-        gains(first)
+        gains(first, nc.gpsimd)
         normalise(0, 0, "gpsimd")
         normalise(0, 1, "gpsimd")
         squares(3)
@@ -308,23 +314,24 @@ def tile_yuyipointupdate_pb_kernel(tc, h1, W2_words, W2_scales, g2, b2, out):
         measure(3, 3)
         aggregate(2)
         aggregate(3)
+        mean_times_g2(second, nc.vector)
         normalise(2, 0, "scalar")
         normalise(2, 1, "vector")
+        normalise(3, 0, "scalar")
         reciprocal_roots(second)
         turn_half(0, 0, (0, 1))
-        gains(second)
-        normalise(3, 0, "scalar")
+        gains(second, nc.vector)
         normalise(0, 2, "vector")
         normalise(0, 3, "vector")
-        leave_half(0, 0, 0)
         normalise(3, 1, "scalar")
-        normalise(2, 2, "vector")
+        leave_half(0, 0, 0)
         leave_half(0, 0, 1)
         turn_half(0, 1, (4, 5))
         normalise(1, 2, "gpsimd")
         normalise(1, 3, "gpsimd")
         normalise(1, 0, "gpsimd")
         normalise(1, 1, "gpsimd")
+        normalise(2, 2, "vector")
         normalise(2, 3, "scalar")
         normalise(3, 3, "vector")
         leave_half(0, 1, 0)

@@ -29,7 +29,7 @@ FLOPS = 2 * GRAPHS * NODES * CHANNELS_IN * CHANNELS_OUT
 
 RUN = 4
 VECTOR_RUNS_EARLY = 64
-VECTOR_RUNS_LATE = 100
+VECTOR_RUNS_LATE = 104
 EARLY_CHUNKS = 4
 WARM_UP = 14
 KEEP_BUSY = 3
@@ -187,11 +187,11 @@ def tile_yuyipointupdate_pb_kernel(tc, h1, W2_words, W2_scales, g2, b2, out):
             multiply(0, t, t)
         regroup(3)
         quantise(2)
+        quantise(3)
         nc.scalar.copy(out=gb[:], in_=gb_bank[:, 0 : 2 * O_TILES])
         move_out(0, 0)
         move_out(0, 1)
         regroup(4)
-        quantise(3)
         for t in range(O_TILES):
             multiply(1, t, O_TILES + t)
         move_out(0, 2)
@@ -205,16 +205,18 @@ def tile_yuyipointupdate_pb_kernel(tc, h1, W2_words, W2_scales, g2, b2, out):
         regroup(7)
         quantise(6)
         quantise(7)
-        for tiles in (first, second):
-            for t in range(tiles.start, tiles.stop):
-                move_out(1, t)
-            means(tiles)
+        move_out(1, 0)
+        move_out(1, 1)
+        means(first)
+        move_out(1, 2)
+        move_out(1, 3)
+        means(second)
         for t in range(O_TILES):
             multiply(3, t, O_TILES + t, KEEP_BUSY if t == O_TILES - 1 else 1)
 
         rstd = keep.tile([P, O_TILES], F32, name="rstd")
         gain = keep.tile([P, O_TILES], F32, name="gain")
-        mean_g2 = {h: keep.tile([P, O_TILES // 2], F32, name="mean_g2_%d" % h) for h in (0, 2)}
+        mean_g2 = keep.tile([P, O_TILES], F32, name="mean_g2")
         mean_gain = keep.tile([P, O_TILES], F32, name="mean_gain")
         shift = keep.tile([P, O_TILES], F32, name="shift")
 
@@ -224,13 +226,13 @@ def tile_yuyipointupdate_pb_kernel(tc, h1, W2_words, W2_scales, g2, b2, out):
         def reciprocal_roots(tiles):
             nc.scalar.activation(out=rstd[:, tiles], in_=mean_var[:, tiles, 1], func=ACT.Abs_reciprocal_sqrt, bias=eps[:])
 
-        def mean_times_g2(tiles, builder):
-            builder.tensor_mul(out=mean_g2[tiles.start][:], in0=mean_var[:, tiles, 0], in1=gb[:, tiles])
+        def mean_times_g2(tiles):
+            nc.vector.tensor_mul(out=mean_g2[:, tiles], in0=mean_var[:, tiles, 0], in1=gb[:, tiles])
 
-        def gains(tiles, builder):
-            builder.tensor_mul(out=mean_gain[:, tiles], in0=mean_g2[tiles.start][:], in1=rstd[:, tiles])
-            builder.tensor_mul(out=gain[:, tiles], in0=gb[:, tiles], in1=rstd[:, tiles])
-            builder.tensor_sub(
+        def gains(tiles):
+            nc.vector.tensor_mul(out=mean_gain[:, tiles], in0=mean_g2[:, tiles], in1=rstd[:, tiles])
+            nc.vector.tensor_mul(out=gain[:, tiles], in0=gb[:, tiles], in1=rstd[:, tiles])
+            nc.vector.tensor_sub(
                 out=shift[:, tiles],
                 in0=gb[:, O_TILES + tiles.start : O_TILES + tiles.stop],
                 in1=mean_gain[:, tiles],
@@ -302,11 +304,11 @@ def tile_yuyipointupdate_pb_kernel(tc, h1, W2_words, W2_scales, g2, b2, out):
         squares(2)
         aggregate(0)
         aggregate(1)
-        mean_times_g2(first, nc.gpsimd)
+        mean_times_g2(first)
         reciprocal_roots(first)
         keep_means(second)
         measure(2, 3)
-        gains(first, nc.gpsimd)
+        gains(first)
         normalise(0, 0, "gpsimd")
         normalise(0, 1, "gpsimd")
         squares(3)
@@ -314,13 +316,13 @@ def tile_yuyipointupdate_pb_kernel(tc, h1, W2_words, W2_scales, g2, b2, out):
         measure(3, 3)
         aggregate(2)
         aggregate(3)
-        mean_times_g2(second, nc.vector)
+        mean_times_g2(second)
         normalise(2, 0, "scalar")
         normalise(2, 1, "vector")
         normalise(3, 0, "scalar")
         reciprocal_roots(second)
         turn_half(0, 0, (0, 1))
-        gains(second, nc.vector)
+        gains(second)
         normalise(0, 2, "vector")
         normalise(0, 3, "vector")
         normalise(3, 1, "scalar")

@@ -28,11 +28,10 @@ NEG_SLOPE = 0.01
 FLOPS = 2 * GRAPHS * NODES * CHANNELS_IN * CHANNELS_OUT
 
 RUN = 4
-VECTOR_RUNS_EARLY = 64
+VECTOR_RUNS_EARLY = 72
 VECTOR_RUNS_LATE = 104
 EARLY_CHUNKS = 4
 WARM_UP = 14
-KEEP_BUSY = 3
 SCALAR_GRAPHS = 2
 TRIPLE = 3
 STATS_WIDTH = TRIPLE + (GRAPHS - SCALAR_GRAPHS) * 2 * TRIPLE
@@ -123,9 +122,9 @@ def tile_yuyipointupdate_pb_kernel(tc, h1, W2_words, W2_scales, g2, b2, out):
                 in_=grouped[c][:].rearrange("p n t -> p (n t)"),
             )
 
-        def multiply(b, t, k, times=1):
+        def multiply(b, t, k):
             z[b, t] = bank(k, [P, NODES], F32, "z")
-            for g in list(range(PASSES)) * times:
+            for g in range(PASSES):
                 nc.tensor.matmul_mx(
                     out=z[b, t][:],
                     lhsT=w_words[:, g, 2 * P * t : 2 * P * (t + 1)].bitcast(FP4X4),
@@ -212,7 +211,7 @@ def tile_yuyipointupdate_pb_kernel(tc, h1, W2_words, W2_scales, g2, b2, out):
         move_out(1, 3)
         means(second)
         for t in range(O_TILES):
-            multiply(3, t, O_TILES + t, KEEP_BUSY if t == O_TILES - 1 else 1)
+            multiply(3, t, O_TILES + t)
 
         rstd = keep.tile([P, O_TILES], F32, name="rstd")
         gain = keep.tile([P, O_TILES], F32, name="gain")
@@ -326,6 +325,7 @@ def tile_yuyipointupdate_pb_kernel(tc, h1, W2_words, W2_scales, g2, b2, out):
         normalise(0, 2, "vector")
         normalise(0, 3, "vector")
         normalise(3, 1, "scalar")
+        normalise(2, 2, "vector")
         leave_half(0, 0, 0)
         leave_half(0, 0, 1)
         turn_half(0, 1, (4, 5))
@@ -333,10 +333,9 @@ def tile_yuyipointupdate_pb_kernel(tc, h1, W2_words, W2_scales, g2, b2, out):
         normalise(1, 3, "gpsimd")
         normalise(1, 0, "gpsimd")
         normalise(1, 1, "gpsimd")
-        normalise(2, 2, "vector")
         normalise(2, 3, "scalar")
-        normalise(3, 3, "vector")
         leave_half(0, 1, 0)
+        normalise(3, 3, "vector")
         normalise(3, 2, "scalar")
         leave_half(0, 1, 1)
         turn(2, (2, 3, 6, 7))

from contextlib import ExitStack

import concourse.masks as masks
import concourse.mybir as mybir

BF16 = mybir.dt.bfloat16
F32 = mybir.dt.float32
I32 = mybir.dt.int32
U8 = mybir.dt.uint8
U32 = mybir.dt.uint32
FP8X4 = mybir.dt.float8_e4m3fn_x4
FP4X4 = mybir.dt.float4_e2m1fn_x4
ALU = mybir.AluOpType
ACT = mybir.ActivationFunctionType

P = 128
PACK = 4
K_PASS = P * PACK

GRAPHS, CHANNELS_IN, NODES, CHANNELS_OUT = 4, 1024, 512, 512
PASSES = CHANNELS_IN // K_PASS
O_TILES = CHANNELS_OUT // P
N_TILES = NODES // P
UNITS = GRAPHS * O_TILES
EPS_BN = 1e-5
NEG_SLOPE = 0.01

FLOPS = 2 * GRAPHS * NODES * CHANNELS_IN * CHANNELS_OUT

RUN = 4
VECTOR_RUNS_EARLY = 72
VECTOR_RUNS_LATE = 104
EARLY_CHUNKS = 4
WARM_UP = 14
SCALAR_GRAPHS = 2
TRIPLE = 3
STATS_WIDTH = TRIPLE + (GRAPHS - SCALAR_GRAPHS) * 2 * TRIPLE


def tile_yuyipointupdate_pb_kernel(tc, h1, W2_words, W2_scales, g2, b2, out):
    nc = tc.nc
    with ExitStack() as ctx:
        keep = ctx.enter_context(tc.tile_pool(name="keep", bufs=1))
        group_pool = ctx.enter_context(tc.tile_pool(name="group", bufs=3))
        work = ctx.enter_context(tc.tile_pool(name="work", bufs=8))
        psum = ctx.enter_context(tc.psum_pool(name="psum", bufs=1))
        ctx.enter_context(tc.manual_schedule())

        def bank(k, shape, dtype, name):
            return psum.tile(shape, dtype, tag="bank%d" % k, name=name)

        identity = keep.tile([P, P], F32, name="identity")
        masks.make_identity(nc, identity[:])
        raw = {}
        w_planes = keep.tile([P, PASSES, CHANNELS_OUT], U8, name="w_planes", align_bytes=64)
        nc.vector.memset(w_planes[:].bitcast(I32), 0)
        gb_rows = keep.tile([2 * O_TILES, P], BF16, name="gb_rows")
        w_words = keep.tile([P, PASSES, 2 * CHANNELS_OUT], U8, name="w_words", align_bytes=64)
        for c in range(GRAPHS * PASSES):
            b, g = c // PASSES, c % PASSES
            raw[c] = keep.tile([P, PACK, NODES], BF16, name="raw_%d" % c)
            rows = h1[b, g * K_PASS : (g + 1) * K_PASS, :]
            nc.sync.dma_start(out=raw[c][:], in_=rows.rearrange("(p t) n -> p t n", t=PACK))
            if c == 1:
                nc.sync.dma_start(out=gb_rows[0:O_TILES, :], in_=g2.rearrange("(t m) -> t m", m=P))
                nc.sync.dma_start(out=gb_rows[O_TILES : 2 * O_TILES, :], in_=b2.rearrange("(t m) -> t m", m=P))
            if c == 3:
                for quadrant in range(4):
                    nc.sync.dma_start(
                        out=w_planes[32 * quadrant : 32 * quadrant + 4, :, :].bitcast(I32),
                        in_=W2_scales.bitcast(I32)[:, 4 * quadrant : 4 * quadrant + 4, :].rearrange("g r m -> r g m"),
                    )
                nc.sync.dma_start(out=w_words[:].bitcast(I32), in_=W2_words.bitcast(I32).rearrange("g p m -> p g m"))

        eps = keep.tile([P, 1], F32, name="eps")
        nc.vector.memset(eps[:], EPS_BN)
        warm = keep.tile([P, 1], F32, name="warm")
        nc.scalar.activation(out=warm[:], in_=eps[:], func=ACT.Abs_reciprocal_sqrt)
        gb_square = keep.tile([P, P], F32, name="gb_square")
        nc.vector.memset(gb_square[:], 0.0)
        gb = keep.tile([P, 2 * O_TILES], F32, name="gb")

        stats = keep.tile([P, O_TILES, STATS_WIDTH], F32, name="stats")
        nc.vector.memset(stats[:, :, 0:1], float(SCALAR_GRAPHS * NODES))
        sums = keep.tile([P, SCALAR_GRAPHS, O_TILES], F32, name="sums")
        both = keep.tile([P, O_TILES], F32, name="both")
        mean = keep.tile([P, O_TILES], F32, name="mean")
        z_kept = [keep.tile([P, SCALAR_GRAPHS, NODES], F32, name="z_kept_%d" % t) for t in range(O_TILES)]
        mean_var = keep.tile([P, O_TILES, 2], F32, name="mean_var")

        idle_bank = bank(6, [P, P], F32, "idle_bank")
        for i in range(WARM_UP):
            nc.tensor.matmul(out=idle_bank[:], lhsT=identity[:], rhs=identity[:], start=True, stop=True)

        grouped = {}
        codes = {}
        planes = {}
        z = {}
        z_sb = {}
        y = {}

        def vector_runs(c):
            return VECTOR_RUNS_EARLY if c < EARLY_CHUNKS else VECTOR_RUNS_LATE

        def regroup_vector(c):
            grouped[c] = group_pool.tile([P, NODES, PACK], BF16, name="grouped", align_bytes=64)
            src = raw[c][:].rearrange("p t (c i) -> p c t i", i=RUN)
            dst = grouped[c][:].rearrange("p (c i) t -> p c t i", i=RUN)
            nc.vector.tensor_copy(out=dst[:, : vector_runs(c)], in_=src[:, : vector_runs(c)])

        def regroup_scalar(c):
            src = raw[c][:].rearrange("p t (c i) -> p c t i", i=RUN)
            dst = grouped[c][:].rearrange("p (c i) t -> p c t i", i=RUN)
            nc.scalar.copy(out=dst[:, vector_runs(c) :], in_=src[:, vector_runs(c) :])

        def quantise(c):
            codes[c] = keep.tile([P, NODES], U32, name="codes_%d" % c, align_bytes=64)
            planes[c] = keep.tile([P, NODES], U8, name="planes_%d" % c, align_bytes=64)
            nc.vector.quantize_mx(
                out=codes[c][:].bitcast(FP8X4),
                scales=planes[c][:],
                in_=grouped[c][:].rearrange("p n t -> p (n t)"),
            )

        def multiply(b, t, k):
            z[b, t] = bank(k, [P, NODES], F32, "z")
            for g in range(PASSES):
                nc.tensor.matmul_mx(
                    out=z[b, t][:],
                    lhsT=w_words[:, g, 2 * P * t : 2 * P * (t + 1)].bitcast(FP4X4),
                    lhsT_scale=w_planes[:, g, P * t : P * (t + 1)],
                    rhs=codes[b * PASSES + g][:].bitcast(FP8X4),
                    rhs_scale=planes[b * PASSES + g][:],
                    start=(g == 0),
                    stop=(g == PASSES - 1),
                )

        def move_out(b, t):
            z_sb[b, t] = z_kept[t][:, b, :]
            nc.scalar.activation(out=z_sb[b, t], in_=z[b, t][:], func=ACT.Copy, accum_out=sums[:, b, t : t + 1])

        def means(tiles):
            nc.gpsimd.tensor_tensor(out=both[:, tiles], in0=sums[:, 0, tiles], in1=sums[:, 1, tiles], op=ALU.add)
            nc.gpsimd.tensor_scalar(
                out=mean[:, tiles],
                in0=both[:, tiles],
                scalar1=1.0 / (SCALAR_GRAPHS * NODES),
                scalar2=0.0,
                op0=ALU.mult,
                op1=ALU.add,
            )

        def keep_means(tiles):
            nc.scalar.copy(out=stats[:, tiles, 1], in_=mean[:, tiles])

        def squares(t):
            junk = work.tile([P, SCALAR_GRAPHS, NODES], F32, name="junk")
            nc.scalar.activation(
                out=junk[:],
                in_=z_kept[t][:],
                func=ACT.Square,
                scale=-1.0,
                bias=mean[:, t : t + 1],
                accum_out=stats[:, t, 2:3],
            )

        def measure(b, t):
            start = TRIPLE + (b - SCALAR_GRAPHS) * 2 * TRIPLE
            nc.vector.bn_stats(out=stats[:, t, start : start + 2 * TRIPLE], in_=z[b, t][:])

        first, second = slice(0, 2), slice(2, 4)

        def regroup(c):
            regroup_vector(c)
            regroup_scalar(c)

        regroup(0)
        regroup(1)
        quantise(0)
        nc.scalar.copy(out=gb_square[0 : 2 * O_TILES, :], in_=gb_rows[:])
        gb_bank = bank(7, [P, P], F32, "gb_bank")
        nc.tensor.transpose(gb_bank[:], gb_square[:], identity[:])
        regroup(2)
        quantise(1)
        for t in range(O_TILES):
            multiply(0, t, t)
        regroup(3)
        quantise(2)
        quantise(3)
        nc.scalar.copy(out=gb[:], in_=gb_bank[:, 0 : 2 * O_TILES])
        move_out(0, 0)
        move_out(0, 1)
        regroup(4)
        for t in range(O_TILES):
            multiply(1, t, O_TILES + t)
        move_out(0, 2)
        move_out(0, 3)
        regroup(5)
        quantise(4)
        regroup(6)
        quantise(5)
        for t in range(O_TILES):
            multiply(2, t, t)
        regroup(7)
        quantise(6)
        quantise(7)
        move_out(1, 0)
        move_out(1, 1)
        means(first)
        move_out(1, 2)
        move_out(1, 3)
        means(second)
        for t in range(O_TILES):
            multiply(3, t, O_TILES + t)

        rstd = keep.tile([P, O_TILES], F32, name="rstd")
        gain = keep.tile([P, O_TILES], F32, name="gain")
        mean_g2 = keep.tile([P, O_TILES], F32, name="mean_g2")
        mean_gain = keep.tile([P, O_TILES], F32, name="mean_gain")
        shift = keep.tile([P, O_TILES], F32, name="shift")

        def aggregate(t):
            nc.vector.bn_aggr(out=mean_var[:, t, :], in_=stats[:, t, :])

        def reciprocal_roots(tiles):
            nc.scalar.activation(out=rstd[:, tiles], in_=mean_var[:, tiles, 1], func=ACT.Abs_reciprocal_sqrt, bias=eps[:])

        def mean_times_g2(tiles):
            nc.vector.tensor_mul(out=mean_g2[:, tiles], in0=mean_var[:, tiles, 0], in1=gb[:, tiles])

        def gains(tiles):
            nc.vector.tensor_mul(out=mean_gain[:, tiles], in0=mean_g2[:, tiles], in1=rstd[:, tiles])
            nc.vector.tensor_mul(out=gain[:, tiles], in0=gb[:, tiles], in1=rstd[:, tiles])
            nc.vector.tensor_sub(
                out=shift[:, tiles],
                in0=gb[:, O_TILES + tiles.start : O_TILES + tiles.stop],
                in1=mean_gain[:, tiles],
            )

        turned = {}

        def normalise(b, t, engine):
            if b not in y:
                y[b] = keep.tile([P, O_TILES, NODES], F32, name="y_%d" % b, tag="y_%d" % (0 if b == 1 else b))
            source = z_sb[b, t] if (b, t) in z_sb else z[b, t][:]
            if engine == "scalar":
                nc.scalar.activation(
                    out=y[b][:, t, :], in_=source, func=ACT.Identity, bias=shift[:, t : t + 1], scale=gain[:, t : t + 1]
                )
            else:
                builder = nc.vector if engine == "vector" else nc.gpsimd
                builder.tensor_scalar(
                    out=y[b][:, t, :],
                    in0=source,
                    scalar1=gain[:, t : t + 1],
                    scalar2=shift[:, t : t + 1],
                    op0=ALU.mult,
                    op1=ALU.add,
                )

        def turn(b, banks):
            for j in range(N_TILES):
                turned[b, j] = bank(banks[j], [P, CHANNELS_OUT], F32, "turned")
                for t in range(O_TILES):
                    nc.tensor.transpose(turned[b, j][:, t * P : (t + 1) * P], y[b][:, t, j * P : (j + 1) * P], identity[:])

        def leave(b, j):
            sloped = work.tile([P, CHANNELS_OUT], F32, name="sloped")
            nc.scalar.mul(out=sloped[:], in_=turned[b, j][:], mul=NEG_SLOPE)
            result = work.tile([P, CHANNELS_OUT], F32, name="result")
            nc.vector.tensor_tensor(out=result[:], in0=turned[b, j][:], in1=sloped[:], op=ALU.max)
            nc.sync.dma_start(out=out[b, j * P : (j + 1) * P, :], in_=result[:])

        def turn_half(b, half, banks):
            for i in range(2):
                turned[b, half, i] = bank(banks[i], [P, 2, 2 * P], F32, "turned_half")
                for t in range(2):
                    for j in range(2):
                        nc.tensor.transpose(
                            turned[b, half, i][:, j, t * P : (t + 1) * P],
                            y[b][:, 2 * half + t, (2 * i + j) * P : (2 * i + j + 1) * P],
                            identity[:],
                        )

        def leave_half(b, half, i):
            sloped = work.tile([P, 2, 2 * P], F32, name="sloped_half")
            nc.scalar.mul(out=sloped[:], in_=turned[b, half, i][:], mul=NEG_SLOPE)
            result = work.tile([P, 2, 2 * P], F32, name="result_half")
            nc.vector.tensor_tensor(out=result[:], in0=turned[b, half, i][:], in1=sloped[:], op=ALU.max)
            nc.sync.dma_start(
                out=out[b, 2 * i * P : 2 * (i + 1) * P, 2 * half * P : 2 * (half + 1) * P].rearrange("(j p) c -> p j c", p=P),
                in_=result[:],
            )

        measure(2, 0)
        squares(0)
        measure(2, 1)
        squares(1)
        keep_means(first)
        measure(3, 0)
        measure(3, 1)
        measure(2, 2)
        squares(2)
        aggregate(0)
        aggregate(1)
        mean_times_g2(first)
        reciprocal_roots(first)
        keep_means(second)
        measure(2, 3)
        gains(first)
        normalise(0, 0, "gpsimd")
        normalise(0, 1, "gpsimd")
        squares(3)
        measure(3, 2)
        measure(3, 3)
        aggregate(2)
        aggregate(3)
        mean_times_g2(second)
        normalise(2, 0, "scalar")
        normalise(2, 1, "vector")
        normalise(3, 0, "scalar")
        reciprocal_roots(second)
        turn_half(0, 0, (0, 1))
        gains(second)
        normalise(0, 2, "vector")
        normalise(0, 3, "vector")
        normalise(3, 1, "scalar")
        normalise(2, 2, "vector")
        leave_half(0, 0, 0)
        leave_half(0, 0, 1)
        turn_half(0, 1, (4, 5))
        normalise(1, 2, "gpsimd")
        normalise(1, 3, "gpsimd")
        normalise(1, 0, "gpsimd")
        normalise(1, 1, "gpsimd")
        normalise(2, 3, "scalar")
        leave_half(0, 1, 0)
        normalise(3, 3, "vector")
        normalise(3, 2, "scalar")
        leave_half(0, 1, 1)
        turn(2, (2, 3, 6, 7))
        leave(2, 0)
        leave(2, 1)
        leave(2, 2)
        leave(2, 3)
        turn(3, (0, 1, 4, 5))
        leave(3, 0)
        leave(3, 1)
        leave(3, 2)
        leave(3, 3)
        turn(1, (2, 3, 6, 7))
        leave(1, 0)
        leave(1, 1)
        leave(1, 2)
        leave(1, 3)
